import numpy as np
import ml_dtypes


def mxq(x, axis, fmt="e4m3"):
    dtype, down = {"e4m3": (ml_dtypes.float8_e4m3fn, 7), "e5m2": (ml_dtypes.float8_e5m2, 14)}[fmt]
    v = np.moveaxis(np.asarray(x, np.float32).astype(ml_dtypes.bfloat16).astype(np.float64), axis, -1)
    blocks = v.reshape(v.shape[:-1] + (-1, 32))
    amax = np.abs(blocks).max(-1, keepdims=True)
    byte = np.maximum(np.where(amax > 0, np.frexp(amax)[1] - 1 + 127, 0) - down, 1)
    scale = np.exp2(byte - 127.0)
    codes = (blocks / scale).astype(np.float32).astype(dtype).astype(np.float64)
    return np.moveaxis((codes * scale).reshape(v.shape), -1, axis)


WIDE = False


def mx_kscale(k):
    if not WIDE:
        return np.ones(k)
    levels = np.array([10, -10, 5, -5, 0])
    a = np.random.permutation(np.resize(levels, k // 512 * 4)).reshape(k // 512, 4)
    idx = np.arange(k)
    return np.exp2(a[idx // 512, idx % 128 // 32])


BF16 = ml_dtypes.bfloat16


def bf(x):
    return np.asarray(x, np.float32).astype(BF16)


def f64(x):
    return np.asarray(x).astype(np.float64)


B, S, H, D, T = 16, 512, 2, 128, 512
QK_STD, V_STD = 1.2, 2.0


def setup_inputs():
    std = np.array([QK_STD, QK_STD, V_STD])[None, None, :, None, None]
    x = np.random.standard_normal((B, S, 3, H, D)) * std
    s = np.array(mx_kscale(S), dtype=np.float64)
    s[:T // 4] = s.min()
    x[:, :, 0, :, 0] = np.sqrt(D) * np.log(2.0)
    x[:, :, 1, :, 0] -= np.log2(s)[None, :, None]
    x[:, :, 2] *= (s / s.min())[None, :, None, None]
    return {"qkv": bf(x)}


def reference(qkv):
    x = f64(qkv)
    softmax_scale = D ** (-0.5)
    q = np.ascontiguousarray(x[:, :, 0].transpose(0, 2, 1, 3))
    k = np.ascontiguousarray(x[:, :, 1].transpose(0, 2, 1, 3))
    v = np.ascontiguousarray(x[:, :, 2].transpose(0, 2, 1, 3))
    vq = mxq(v, 2, "e4m3")
    out = np.zeros((B, H, S, D))
    for i in range(S // T):
        r0, n = i * T, (i + 1) * T
        scores = q[:, :, r0:n] @ k[:, :, :n].transpose(0, 1, 3, 2) * softmax_scale
        causal = np.arange(r0, n)[:, None] >= np.arange(n)[None, :]
        scores = np.where(causal[None, None, :, :], scores, -1000000000.0)
        e = np.exp(scores - scores.max(-1, keepdims=True))
        out[:, :, r0:n] = (mxq(e, 3, "e4m3") @ vq[:, :, :n]) / e.sum(-1, keepdims=True)
    return out.transpose(0, 2, 1, 3)

@@ -1,0 +1,202 @@
+from contextlib import ExitStack
+
+import concourse.mybir as mybir
+from concourse.masks import make_identity
+
+BF16 = mybir.dt.bfloat16
+F32 = mybir.dt.float32
+U32 = mybir.dt.uint32
+U8 = mybir.dt.uint8
+FP8X4 = mybir.dt.float8_e4m3fn_x4
+ACT = mybir.ActivationFunctionType
+ALU = mybir.AluOpType
+AX = mybir.AxisListType
+
+B, S, H, D = 16, 512, 2, 128
+P = 128
+NCH = S // P
+PACK = 4
+NX = NCH * H
+SCALE = D ** -0.5
+NEG = -1.0e9
+NSET = 2
+FLOPS = 4 * B * H * S * S * D
+
+
+def tile_causalselfattention_t_kernel(tc, qkv, out):
+    nc = tc.nc
+    with ExitStack() as ctx:
+        const = ctx.enter_context(tc.tile_pool(name="const", bufs=1))
+        inp = ctx.enter_context(tc.tile_pool(name="inp", bufs=B))
+        work = ctx.enter_context(tc.tile_pool(name="work", bufs=2))
+        small = ctx.enter_context(tc.tile_pool(name="small", bufs=3))
+        ps_tq = ctx.enter_context(tc.psum_pool(name="ps_tq", bufs=1))
+        ps_s = ctx.enter_context(tc.psum_pool(name="ps_s", bufs=3))
+        ps_xt = ctx.enter_context(tc.psum_pool(name="ps_xt", bufs=2))
+        ps_o = ctx.enter_context(tc.psum_pool(name="ps_o", bufs=2))
+
+        qk_sb = []
+        v_sb = []
+        for b in range(B):
+            qk = inp.tile([P, NCH, 2 * H * D], BF16, tag="qk")
+            nc.sync.dma_start(
+                out=qk[:], in_=qkv[b, :, 0:2, :, :].rearrange("(c p) w h d -> p c (w h d)", p=P)
+            )
+            v = inp.tile([P, PACK, H * D], BF16, tag="v")
+            nc.sync.dma_start(
+                out=v[:], in_=qkv[b, :, 2, :, :].rearrange("(p t) h d -> p t (h d)", t=PACK)
+            )
+            qk_sb.append(qk)
+            v_sb.append(v)
+
+        ident = const.tile([P, P], BF16, name="ident")
+        make_identity(nc, ident[:])
+        maskf = const.tile([P, P], F32, name="maskf")
+        nc.gpsimd.memset(maskf[:], 0.0)
+        nc.gpsimd.affine_select(
+            out=maskf[:],
+            in_=maskf[:],
+            pattern=[[-1, P]],
+            compare_op=ALU.is_ge,
+            fill=NEG,
+            base=0,
+            channel_multiplier=1,
+        )
+        maskb = const.tile([P, P], BF16, name="maskb")
+        nc.vector.tensor_copy(out=maskb[:], in_=maskf[:])
+
+        e_tiles = []
+        for s_i in range(NSET):
+            row = []
+            for x in range(NX):
+                e_t = const.tile([P, PACK, P], BF16, name="e_%d_%d" % (s_i, x))
+                live = (P // PACK) * (x // H + 1)
+                if live < P:
+                    nc.vector.memset(e_t[:, :, live:P], 0.0)
+                row.append(e_t)
+            e_tiles.append(row)
+
+        state = {}
+
+        def front(b):
+            vg = work.tile([P, H * D, PACK], BF16, tag="vg", align_bytes=64)
+            nc.vector.tensor_copy(out=vg[:], in_=v_sb[b][:].rearrange("p t c -> p c t"))
+            vw = work.tile([P, H * D], U32, tag="vw", align_bytes=64)
+            vp = work.tile([P, H * D], U8, tag="vp", align_bytes=64)
+            nc.vector.quantize_mx(
+                out=vw[:].bitcast(FP8X4), scales=vp[:], in_=vg[:].rearrange("p c t -> p (c t)")
+            )
+            nm = small.tile([P, NX], F32, tag="nm")
+            bias = small.tile([P, NX], F32, tag="bias")
+            rs = small.tile([P, NX], F32, tag="rs")
+            qkT = []
+            for h in range(H):
+                tq = ps_tq.tile([P, 2 * NCH, P], BF16, tag="tq")
+                for w in range(2):
+                    for c in range(NCH):
+                        col = (w * H + h) * D
+                        nc.tensor.transpose(
+                            out=tq[:, w * NCH + c, :],
+                            in_=qk_sb[b][:, c, col : col + D],
+                            identity=ident[:],
+                        )
+                qt = work.tile([P, 2 * NCH, P], BF16, tag="qkT%d" % h)
+                nc.vector.tensor_copy(out=qt[:], in_=tq[:])
+                qkT.append(qt)
+            for ic in range(NCH):
+                for h in range(H):
+                    x = ic * H + h
+                    j_n = P * (ic + 1)
+                    s_ps = ps_s.tile([P, S], F32, tag="s")
+                    nc.tensor.matmul(
+                        out=s_ps[:, 0:j_n],
+                        lhsT=qkT[h][:, ic, :],
+                        rhs=qkT[h][:, NCH : NCH + ic + 1, :].rearrange("p c j -> p (c j)"),
+                        start=True,
+                        stop=False,
+                    )
+                    nc.tensor.matmul(
+                        out=s_ps[:, j_n - P : j_n],
+                        lhsT=ident[:],
+                        rhs=maskb[:],
+                        start=False,
+                        stop=True,
+                    )
+                    nc.vector.tensor_reduce(
+                        out=nm[:, x : x + 1], in_=s_ps[:, 0:j_n], axis=AX.X, op=ALU.max, negate=True
+                    )
+                    nc.gpsimd.tensor_scalar(
+                        out=bias[:, x : x + 1],
+                        in0=nm[:, x : x + 1],
+                        scalar1=SCALE,
+                        scalar2=0.0,
+                        op0=ALU.mult,
+                        op1=ALU.add,
+                    )
+                    nc.scalar.activation(
+                        out=e_tiles[b % NSET][x][:, :, 0 : j_n // PACK],
+                        in_=s_ps[:, 0:j_n].rearrange("i (p t) -> i t p", t=PACK),
+                        func=ACT.Exp,
+                        bias=bias[:, x : x + 1],
+                        scale=SCALE,
+                        accum_out=rs[:, x : x + 1],
+                    )
+            state[b] = (vw, vp, rs)
+
+        def back(b):
+            vw, vp, rs = state[b]
+            g = work.tile([P, NX, P, PACK], BF16, tag="g", align_bytes=64)
+            ew = work.tile([P, NX * P], U32, tag="ew", align_bytes=64)
+            ep = work.tile([P, NX * P], U8, tag="ep", align_bytes=64)
+            for j in range(NCH):
+                xt = ps_xt.tile([P, H, PACK, P], BF16, tag="xt")
+                for h in range(H):
+                    for t in range(PACK):
+                        nc.tensor.transpose(
+                            out=xt[:, h, t, :],
+                            in_=e_tiles[b % NSET][j * H + h][:, t, :],
+                            identity=ident[:],
+                        )
+                nc.scalar.copy(
+                    out=g[:, j * H : (j + 1) * H, :, :], in_=xt[:].rearrange("p x t i -> p x i t")
+                )
+                lo = j * H * P
+                hi = (j + 1) * H * P
+                nc.vector.quantize_mx(
+                    out=ew[:, lo:hi].bitcast(FP8X4),
+                    scales=ep[:, lo:hi],
+                    in_=g[:, j * H : (j + 1) * H, :, :].rearrange("p x i t -> p (x i t)"),
+                )
+            rinv = small.tile([P, NX], F32, tag="rinv")
+            nc.vector.reciprocal(out=rinv[:], in_=rs[:])
+            o_sb = work.tile([P, NX, D], F32, tag="o_sb")
+            for j2 in range(2):
+                o_ps = ps_o.tile([P, 4, D], F32, tag="o")
+                for x4 in range(4):
+                    x = 4 * j2 + x4
+                    h = x % H
+                    nc.tensor.matmul_mx(
+                        out=o_ps[:, x4, :],
+                        lhsT=ew[:, x * P : (x + 1) * P].bitcast(FP8X4),
+                        lhsT_scale=ep[:, x * P : (x + 1) * P],
+                        rhs=vw[:, h * D : (h + 1) * D].bitcast(FP8X4),
+                        rhs_scale=vp[:, h * D : (h + 1) * D],
+                        start=True,
+                        stop=True,
+                    )
+                nc.vector.tensor_tensor(
+                    out=o_sb[:, 4 * j2 : 4 * j2 + 4, :],
+                    in0=o_ps[:],
+                    in1=rinv[:, 4 * j2 : 4 * j2 + 4].unsqueeze(2).to_broadcast([P, 4, D]),
+                    op=ALU.mult,
+                )
+            nc.sync.dma_start(
+                out=out[b].rearrange("(c p) h d -> p c (h d)", p=P),
+                in_=o_sb[:].rearrange("p (c h) d -> p c (h d)", h=H),
+            )
+
+        for step in range(B + 1):
+            if step < B:
+                front(step)
+            if step >= 1:
+                back(step - 1)

@@ -5,6 +5,7 @@ from concourse.masks import make_identity
 
 BF16 = mybir.dt.bfloat16
 F32 = mybir.dt.float32
+I32 = mybir.dt.int32
 U32 = mybir.dt.uint32
 U8 = mybir.dt.uint8
 FP8X4 = mybir.dt.float8_e4m3fn_x4
@@ -16,7 +17,11 @@ B, S, H, D = 16, 512, 2, 128
 P = 128
 NCH = S // P
 PACK = 4
+QUAD = P // PACK
+HALF = P // 2
 NX = NCH * H
+GROUPS = 3
+NG = GROUPS * B
 SCALE = D ** -0.5
 NEG = -1.0e9
 NSET = 2
@@ -26,17 +31,19 @@ FLOPS = 4 * B * H * S * S * D
 def tile_causalselfattention_t_kernel(tc, qkv, out):
     nc = tc.nc
     with ExitStack() as ctx:
+        ctx.enter_context(tc.manual_schedule())
         const = ctx.enter_context(tc.tile_pool(name="const", bufs=1))
         inp = ctx.enter_context(tc.tile_pool(name="inp", bufs=B))
         work = ctx.enter_context(tc.tile_pool(name="work", bufs=2))
         small = ctx.enter_context(tc.tile_pool(name="small", bufs=3))
         ps_tq = ctx.enter_context(tc.psum_pool(name="ps_tq", bufs=1))
-        ps_s = ctx.enter_context(tc.psum_pool(name="ps_s", bufs=3))
+        ps_s = ctx.enter_context(tc.psum_pool(name="ps_s", bufs=4))
         ps_xt = ctx.enter_context(tc.psum_pool(name="ps_xt", bufs=2))
-        ps_o = ctx.enter_context(tc.psum_pool(name="ps_o", bufs=2))
+        ps_o = ctx.enter_context(tc.psum_pool(name="ps_o", bufs=1))
 
         qk_sb = []
         v_sb = []
+        vlo_sb = []
         for b in range(B):
             qk = inp.tile([P, NCH, 2 * H * D], BF16, tag="qk")
             nc.sync.dma_start(
@@ -46,8 +53,14 @@ def tile_causalselfattention_t_kernel(tc, qkv, out):
             nc.sync.dma_start(
                 out=v[:], in_=qkv[b, :, 2, :, :].rearrange("(p t) h d -> p t (h d)", t=PACK)
             )
+            vlo = inp.tile([P, PACK, D], BF16, tag="vlo")
+            nc.sync.dma_start(
+                out=vlo[HALF:P, :, :],
+                in_=qkv[b, 0 : HALF * PACK, 2, 1, :].rearrange("(p t) d -> p t d", t=PACK),
+            )
             qk_sb.append(qk)
             v_sb.append(v)
+            vlo_sb.append(vlo)
 
         ident = const.tile([P, P], BF16, name="ident")
         make_identity(nc, ident[:])
@@ -68,135 +81,255 @@ def tile_causalselfattention_t_kernel(tc, qkv, out):
         e_tiles = []
         for s_i in range(NSET):
             row = []
-            for x in range(NX):
-                e_t = const.tile([P, PACK, P], BF16, name="e_%d_%d" % (s_i, x))
-                live = (P // PACK) * (x // H + 1)
-                if live < P:
-                    nc.vector.memset(e_t[:, :, live:P], 0.0)
+            for k in range(2 * GROUPS):
+                e_t = const.tile([P, PACK, P], BF16, name="e_%d_%d" % (s_i, k))
+                if k == 0:
+                    nc.vector.memset(e_t[:, :, QUAD:HALF], 0.0)
+                    nc.vector.memset(e_t[:, :, HALF + QUAD : P], 0.0)
+                if k in (2, 3):
+                    nc.vector.memset(e_t[:, :, 3 * QUAD : P], 0.0)
                 row.append(e_t)
             e_tiles.append(row)
+        vg = const.tile([P, H * D, PACK], BF16, name="vg", align_bytes=64)
+        glo = const.tile([P, H, D, PACK], BF16, name="glo", align_bytes=64)
+        nc.vector.memset(glo[:].rearrange("p x d t -> p (x d t)").bitcast(I32), 0)
 
-        state = {}
+        qkT = {}
+        tq_of = {}
+        vq = {}
+        lq = {}
+        stat = {}
+        s_of = {}
+        xt_of = {}
+        g_of = {}
+        ew_of = {}
+        o_of = {}
+        osb_of = {}
 
-        def front(b):
-            vg = work.tile([P, H * D, PACK], BF16, tag="vg", align_bytes=64)
-            nc.vector.tensor_copy(out=vg[:], in_=v_sb[b][:].rearrange("p t c -> p c t"))
-            vw = work.tile([P, H * D], U32, tag="vw", align_bytes=64)
-            vp = work.tile([P, H * D], U8, tag="vp", align_bytes=64)
+        def units(g):
+            if g == 0:
+                return [(0, 0), (0, 1), (1, 0), (1, 1)]
+            return [(g + 1, 0), (g + 1, 1)]
+
+        def regroup(dst, src):
+            nc.gpsimd.tensor_scalar(
+                out=dst, in0=src, scalar1=1.0, scalar2=0.0, op0=ALU.mult, op1=ALU.add
+            )
+
+        def regroup_full(b):
+            regroup(vg[:], v_sb[b][:].rearrange("p t c -> p c t"))
+
+        def regroup_low(b):
+            regroup(glo[0:HALF, 0, :, :], v_sb[b][0:HALF, :, 0:D].rearrange("p t d -> p d t"))
+            regroup(glo[HALF:P, 1, :, :], vlo_sb[b][HALF:P, :, :].rearrange("p t d -> p d t"))
+
+        def quantise_full(b):
+            vw = work.tile([P, H * D], U32, tag="vw", bufs=3, align_bytes=64)
+            vp = work.tile([P, H * D], U8, tag="vp", bufs=3, align_bytes=64)
             nc.vector.quantize_mx(
                 out=vw[:].bitcast(FP8X4), scales=vp[:], in_=vg[:].rearrange("p c t -> p (c t)")
             )
-            nm = small.tile([P, NX], F32, tag="nm")
-            bias = small.tile([P, NX], F32, tag="bias")
-            rs = small.tile([P, NX], F32, tag="rs")
-            qkT = []
-            for h in range(H):
-                tq = ps_tq.tile([P, 2 * NCH, P], BF16, tag="tq")
-                for w in range(2):
-                    for c in range(NCH):
-                        col = (w * H + h) * D
-                        nc.tensor.transpose(
-                            out=tq[:, w * NCH + c, :],
-                            in_=qk_sb[b][:, c, col : col + D],
-                            identity=ident[:],
-                        )
-                qt = work.tile([P, 2 * NCH, P], BF16, tag="qkT%d" % h)
-                nc.vector.tensor_copy(out=qt[:], in_=tq[:])
-                qkT.append(qt)
-            for ic in range(NCH):
-                for h in range(H):
-                    x = ic * H + h
-                    j_n = P * (ic + 1)
-                    s_ps = ps_s.tile([P, S], F32, tag="s")
-                    nc.tensor.matmul(
-                        out=s_ps[:, 0:j_n],
-                        lhsT=qkT[h][:, ic, :],
-                        rhs=qkT[h][:, NCH : NCH + ic + 1, :].rearrange("p c j -> p (c j)"),
-                        start=True,
-                        stop=False,
-                    )
-                    nc.tensor.matmul(
-                        out=s_ps[:, j_n - P : j_n],
-                        lhsT=ident[:],
-                        rhs=maskb[:],
-                        start=False,
-                        stop=True,
-                    )
-                    nc.vector.tensor_reduce(
-                        out=nm[:, x : x + 1], in_=s_ps[:, 0:j_n], axis=AX.X, op=ALU.max, negate=True
-                    )
-                    nc.gpsimd.tensor_scalar(
-                        out=bias[:, x : x + 1],
-                        in0=nm[:, x : x + 1],
-                        scalar1=SCALE,
-                        scalar2=0.0,
-                        op0=ALU.mult,
-                        op1=ALU.add,
-                    )
-                    nc.scalar.activation(
-                        out=e_tiles[b % NSET][x][:, :, 0 : j_n // PACK],
-                        in_=s_ps[:, 0:j_n].rearrange("i (p t) -> i t p", t=PACK),
-                        func=ACT.Exp,
-                        bias=bias[:, x : x + 1],
-                        scale=SCALE,
-                        accum_out=rs[:, x : x + 1],
-                    )
-            state[b] = (vw, vp, rs)
+            vq[b] = [vw, vp]
 
-        def back(b):
-            vw, vp, rs = state[b]
-            g = work.tile([P, NX, P, PACK], BF16, tag="g", align_bytes=64)
-            ew = work.tile([P, NX * P], U32, tag="ew", align_bytes=64)
-            ep = work.tile([P, NX * P], U8, tag="ep", align_bytes=64)
-            for j in range(NCH):
-                xt = ps_xt.tile([P, H, PACK, P], BF16, tag="xt")
-                for h in range(H):
-                    for t in range(PACK):
-                        nc.tensor.transpose(
-                            out=xt[:, h, t, :],
-                            in_=e_tiles[b % NSET][j * H + h][:, t, :],
-                            identity=ident[:],
-                        )
-                nc.scalar.copy(
-                    out=g[:, j * H : (j + 1) * H, :, :], in_=xt[:].rearrange("p x t i -> p x i t")
-                )
-                lo = j * H * P
-                hi = (j + 1) * H * P
-                nc.vector.quantize_mx(
-                    out=ew[:, lo:hi].bitcast(FP8X4),
-                    scales=ep[:, lo:hi],
-                    in_=g[:, j * H : (j + 1) * H, :, :].rearrange("p x i t -> p (x i t)"),
-                )
-            rinv = small.tile([P, NX], F32, tag="rinv")
-            nc.vector.reciprocal(out=rinv[:], in_=rs[:])
-            o_sb = work.tile([P, NX, D], F32, tag="o_sb")
-            for j2 in range(2):
-                o_ps = ps_o.tile([P, 4, D], F32, tag="o")
-                for x4 in range(4):
-                    x = 4 * j2 + x4
-                    h = x % H
-                    nc.tensor.matmul_mx(
-                        out=o_ps[:, x4, :],
-                        lhsT=ew[:, x * P : (x + 1) * P].bitcast(FP8X4),
-                        lhsT_scale=ep[:, x * P : (x + 1) * P],
-                        rhs=vw[:, h * D : (h + 1) * D].bitcast(FP8X4),
-                        rhs_scale=vp[:, h * D : (h + 1) * D],
-                        start=True,
-                        stop=True,
+        def quantise_low(b):
+            lw = work.tile([P, H * D], U32, tag="lw", align_bytes=64)
+            lp = work.tile([P, H * D], U8, tag="lp", align_bytes=64)
+            nc.vector.quantize_mx(
+                out=lw[:].bitcast(FP8X4), scales=lp[:], in_=glo[:].rearrange("p x d t -> p (x d t)")
+            )
+            lq[b] = [lw, lp]
+
+        def transpose_qk(b, h):
+            tq = ps_tq.tile([P, 2 * NCH, P], BF16, tag="tq")
+            for w in range(2):
+                for c in range(NCH):
+                    col = (w * H + h) * D
+                    nc.tensor.transpose(
+                        out=tq[:, w * NCH + c, :],
+                        in_=qk_sb[b][:, c, col : col + D],
+                        identity=ident[:],
                     )
-                nc.vector.tensor_tensor(
-                    out=o_sb[:, 4 * j2 : 4 * j2 + 4, :],
-                    in0=o_ps[:],
-                    in1=rinv[:, 4 * j2 : 4 * j2 + 4].unsqueeze(2).to_broadcast([P, 4, D]),
-                    op=ALU.mult,
-                )
-            nc.sync.dma_start(
-                out=out[b].rearrange("(c p) h d -> p c (h d)", p=P),
-                in_=o_sb[:].rearrange("p (c h) d -> p c (h d)", h=H),
+            tq_of[(b, h)] = tq
+
+        def copy_qk(b, h):
+            qt = work.tile([P, 2 * NCH, P], BF16, tag="qkT%d" % h)
+            nc.vector.tensor_copy(out=qt[:], in_=tq_of[(b, h)][:])
+            qkT[(b, h)] = qt
+
+        def one_score(b, h, ic, dst):
+            qt = qkT[(b, h)]
+            j_n = P * (ic + 1)
+            nc.tensor.matmul(
+                out=dst,
+                lhsT=qt[:, ic, :],
+                rhs=qt[:, NCH : NCH + ic + 1, :].rearrange("p c j -> p (c j)"),
+                start=True,
+                stop=False,
+            )
+            nc.tensor.matmul(
+                out=dst[:, j_n - P : j_n], lhsT=ident[:], rhs=maskb[:], start=False, stop=True
             )
 
-        for step in range(B + 1):
-            if step < B:
-                front(step)
-            if step >= 1:
-                back(step - 1)
+        def scores(n):
+            b, g = divmod(n, GROUPS)
+            if g == 0:
+                nm = small.tile([P, NX], F32, tag="nm")
+                bias = small.tile([P, NX], F32, tag="bias")
+                rs = small.tile([P, NX], F32, tag="rs")
+                stat[b] = [nm, bias, rs]
+            nm, bias, rs = stat[b][0:3]
+            for k in range(2):
+                if g == 0:
+                    ic = k
+                    x0, x1 = ic * H, (ic + 1) * H
+                    s_ps = ps_s.tile([P, H, P * (ic + 1)], F32, tag="s")
+                    for h in range(H):
+                        one_score(b, h, ic, s_ps[:, h, :])
+                        s_of[(b, ic, h)] = s_ps[:, h, :]
+                else:
+                    ic = g + 1
+                    x0, x1 = ic * H + k, ic * H + k + 1
+                    s_ps = ps_s.tile([P, P * (ic + 1)], F32, tag="s")
+                    one_score(b, k, ic, s_ps[:])
+                    s_of[(b, ic, k)] = s_ps[:]
+                nc.vector.tensor_reduce(
+                    out=nm[:, x0:x1], in_=s_ps[:], axis=AX.X, op=ALU.max, negate=True
+                )
+                nc.gpsimd.tensor_scalar(
+                    out=bias[:, x0:x1],
+                    in0=nm[:, x0:x1],
+                    scalar1=SCALE,
+                    scalar2=0.0,
+                    op0=ALU.mult,
+                    op1=ALU.add,
+                )
+
+        def exps(n):
+            b, g = divmod(n, GROUPS)
+            nm, bias, rs = stat[b][0:3]
+            for ic, h in units(g):
+                x = ic * H + h
+                live = QUAD * (ic + 1)
+                if g == 0:
+                    dst = e_tiles[b % NSET][ic][:, :, h * HALF : h * HALF + live]
+                else:
+                    dst = e_tiles[b % NSET][2 * g + h][:, :, 0:live]
+                nc.scalar.activation(
+                    out=dst,
+                    in_=s_of[(b, ic, h)].rearrange("i (p t) -> i t p", t=PACK),
+                    func=ACT.Exp,
+                    bias=bias[:, x : x + 1],
+                    scale=SCALE,
+                    accum_out=rs[:, x : x + 1],
+                )
+
+        def transpose_e(n):
+            b, g = divmod(n, GROUPS)
+            xt = ps_xt.tile([P, 2, PACK, P], BF16, tag="xt")
+            for k in range(2):
+                for t in range(PACK):
+                    nc.tensor.transpose(
+                        out=xt[:, k, t, :],
+                        in_=e_tiles[b % NSET][2 * g + k][:, t, :],
+                        identity=ident[:],
+                    )
+            xt_of[n] = xt
+
+        def copy_out(n):
+            grp = work.tile([P, 2, P, PACK], BF16, tag="grp", bufs=3, align_bytes=64)
+            nc.scalar.copy(out=grp[:], in_=xt_of[n][:].rearrange("p x t i -> p x i t"))
+            g_of[n] = grp
+
+        def quantise_e(n):
+            ew = work.tile([P, 2 * P], U32, tag="ew", align_bytes=64)
+            ep = work.tile([P, 2 * P], U8, tag="ep", align_bytes=64)
+            nc.vector.quantize_mx(
+                out=ew[:].bitcast(FP8X4),
+                scales=ep[:],
+                in_=g_of[n][:].rearrange("p x i t -> p (x i t)"),
+            )
+            ew_of[n] = [ew, ep]
+
+        def passes(n):
+            b, g = divmod(n, GROUPS)
+            ew, ep = ew_of[n]
+            vw, vp = vq[b]
+            lw, lp = lq[b]
+            width = H * D if g == 0 else D
+            o_ps = ps_o.tile([P, 2 * width], F32, tag="o")
+            for k in range(2):
+                if g == 0:
+                    rhs, rhs_scale = lw[:], lp[:]
+                else:
+                    rhs, rhs_scale = vw[:, k * D : (k + 1) * D], vp[:, k * D : (k + 1) * D]
+                nc.tensor.matmul_mx(
+                    out=o_ps[:, k * width : (k + 1) * width],
+                    lhsT=ew[:, k * P : (k + 1) * P].bitcast(FP8X4),
+                    lhsT_scale=ep[:, k * P : (k + 1) * P],
+                    rhs=rhs.bitcast(FP8X4),
+                    rhs_scale=rhs_scale,
+                    start=True,
+                    stop=True,
+                )
+            o_of[n] = o_ps
+
+        def normalise(n):
+            b, g = divmod(n, GROUPS)
+            if g == 0:
+                rinv = small.tile([P, NX], F32, tag="rinv")
+                nc.vector.reciprocal(out=rinv[:], in_=stat[b][2][:])
+                stat[b].append(rinv)
+                o_sb = work.tile([P, NX, D], F32, tag="o_sb")
+                osb_of[b] = o_sb
+            rinv = stat[b][3]
+            o_sb = osb_of[b]
+            x0 = units(g)[0][0] * H
+            n_x = len(units(g))
+            nc.vector.tensor_tensor(
+                out=o_sb[:, x0 : x0 + n_x, :],
+                in0=o_of[n][:].rearrange("p (x d) -> p x d", d=D),
+                in1=rinv[:, x0 : x0 + n_x].unsqueeze(2).to_broadcast([P, n_x, D]),
+                op=ALU.mult,
+            )
+            if g == GROUPS - 1:
+                nc.sync.dma_start(
+                    out=out[b].rearrange("(c p) h d -> p c (h d)", p=P),
+                    in_=o_sb[:].rearrange("p (c h) d -> p c (h d)", h=H),
+                )
+
+        def batch_ok(b):
+            return 0 <= b < B
+
+        regroup_full(0)
+        regroup_low(0)
+        for n in range(-6, NG + 3):
+            b0, r = divmod(n, GROUPS)
+            if 0 <= n - 3 < NG:
+                normalise(n - 3)
+            if 0 <= n - 2 < NG:
+                quantise_e(n - 2)
+            if r == 1 and batch_ok(b0 + 1):
+                quantise_full(b0 + 1)
+                if batch_ok(b0 + 2):
+                    regroup_full(b0 + 2)
+            if r == 2 and batch_ok(b0 + 1):
+                quantise_low(b0 + 1)
+                if batch_ok(b0 + 2):
+                    regroup_low(b0 + 2)
+            if r == 1 and batch_ok(b0 + 2):
+                copy_qk(b0 + 2, 0)
+            if r == 2 and batch_ok(b0 + 2):
+                copy_qk(b0 + 2, 1)
+            if 0 <= n + 2 < NG:
+                scores(n + 2)
+            if 0 <= n + 1 < NG:
+                exps(n + 1)
+            if 0 <= n < NG:
+                transpose_e(n)
+                copy_out(n)
+            if 0 <= n - 2 < NG:
+                passes(n - 2)
+            if r == 0 and batch_ok(b0 + 2):
+                transpose_qk(b0 + 2, 0)
+            if r == 1 and batch_ok(b0 + 2):
+                transpose_qk(b0 + 2, 1)

@@ -41,25 +41,25 @@ def tile_causalselfattention_t_kernel(tc, qkv, out):
         ps_xt = ctx.enter_context(tc.psum_pool(name="ps_xt", bufs=2))
         ps_o = ctx.enter_context(tc.psum_pool(name="ps_o", bufs=1))
 
-        qk_sb = []
-        v_sb = []
+        q_sb = []
+        kv_sb = []
         vlo_sb = []
         for b in range(B):
-            qk = inp.tile([P, NCH, 2 * H * D], BF16, tag="qk")
+            q = inp.tile([P, NCH, H * D], BF16, tag="q")
             nc.sync.dma_start(
-                out=qk[:], in_=qkv[b, :, 0:2, :, :].rearrange("(c p) w h d -> p c (w h d)", p=P)
+                out=q[:], in_=qkv[b, :, 0, :, :].rearrange("(c p) h d -> p c (h d)", p=P)
             )
-            v = inp.tile([P, PACK, H * D], BF16, tag="v")
+            kv = inp.tile([P, PACK, 2 * H * D], BF16, tag="kv")
             nc.sync.dma_start(
-                out=v[:], in_=qkv[b, :, 2, :, :].rearrange("(p t) h d -> p t (h d)", t=PACK)
+                out=kv[:], in_=qkv[b, :, 1:3, :, :].rearrange("(p t) w h d -> p t (w h d)", t=PACK)
             )
             vlo = inp.tile([P, PACK, D], BF16, tag="vlo")
             nc.sync.dma_start(
                 out=vlo[HALF:P, :, :],
                 in_=qkv[b, 0 : HALF * PACK, 2, 1, :].rearrange("(p t) d -> p t d", t=PACK),
             )
-            qk_sb.append(qk)
-            v_sb.append(v)
+            q_sb.append(q)
+            kv_sb.append(kv)
             vlo_sb.append(vlo)
 
         ident = const.tile([P, P], BF16, name="ident")
@@ -75,8 +75,8 @@ def tile_causalselfattention_t_kernel(tc, qkv, out):
             base=0,
             channel_multiplier=1,
         )
-        maskb = const.tile([P, P], BF16, name="maskb")
-        nc.vector.tensor_copy(out=maskb[:], in_=maskf[:])
+        maskb = const.tile([P, PACK, QUAD], BF16, name="maskb")
+        nc.vector.tensor_copy(out=maskb[:], in_=maskf[:].rearrange("i (p t) -> i t p", t=PACK))
 
         e_tiles = []
         for s_i in range(NSET):
@@ -117,10 +117,12 @@ def tile_causalselfattention_t_kernel(tc, qkv, out):
             )
 
         def regroup_full(b):
-            regroup(vg[:], v_sb[b][:].rearrange("p t c -> p c t"))
+            regroup(vg[:], kv_sb[b][:, :, H * D : 2 * H * D].rearrange("p t c -> p c t"))
 
         def regroup_low(b):
-            regroup(glo[0:HALF, 0, :, :], v_sb[b][0:HALF, :, 0:D].rearrange("p t d -> p d t"))
+            regroup(
+                glo[0:HALF, 0, :, :], kv_sb[b][0:HALF, :, H * D : H * D + D].rearrange("p t d -> p d t")
+            )
             regroup(glo[HALF:P, 1, :, :], vlo_sb[b][HALF:P, :, :].rearrange("p t d -> p d t"))
 
         def quantise_full(b):
@@ -141,14 +143,14 @@ def tile_causalselfattention_t_kernel(tc, qkv, out):
 
         def transpose_qk(b, h):
             tq = ps_tq.tile([P, 2 * NCH, P], BF16, tag="tq")
-            for w in range(2):
-                for c in range(NCH):
-                    col = (w * H + h) * D
-                    nc.tensor.transpose(
-                        out=tq[:, w * NCH + c, :],
-                        in_=qk_sb[b][:, c, col : col + D],
-                        identity=ident[:],
-                    )
+            for c in range(NCH):
+                nc.tensor.transpose(
+                    out=tq[:, c, :], in_=q_sb[b][:, c, h * D : (h + 1) * D], identity=ident[:]
+                )
+            for t in range(PACK):
+                nc.tensor.transpose(
+                    out=tq[:, NCH + t, :], in_=kv_sb[b][:, t, h * D : (h + 1) * D], identity=ident[:]
+                )
             tq_of[(b, h)] = tq
 
         def copy_qk(b, h):
@@ -158,16 +160,17 @@ def tile_causalselfattention_t_kernel(tc, qkv, out):
 
         def one_score(b, h, ic, dst):
             qt = qkT[(b, h)]
-            j_n = P * (ic + 1)
+            live = QUAD * (ic + 1)
+            dst3 = dst.rearrange("i (t p) -> i t p", t=PACK)
             nc.tensor.matmul(
-                out=dst,
+                out=dst3,
                 lhsT=qt[:, ic, :],
-                rhs=qt[:, NCH : NCH + ic + 1, :].rearrange("p c j -> p (c j)"),
+                rhs=qt[:, NCH : NCH + PACK, 0:live],
                 start=True,
                 stop=False,
             )
             nc.tensor.matmul(
-                out=dst[:, j_n - P : j_n], lhsT=ident[:], rhs=maskb[:], start=False, stop=True
+                out=dst3[:, :, live - QUAD : live], lhsT=ident[:], rhs=maskb[:], start=False, stop=True
             )
 
         def scores(n):
@@ -216,7 +219,7 @@ def tile_causalselfattention_t_kernel(tc, qkv, out):
                     dst = e_tiles[b % NSET][2 * g + h][:, :, 0:live]
                 nc.scalar.activation(
                     out=dst,
-                    in_=s_of[(b, ic, h)].rearrange("i (p t) -> i t p", t=PACK),
+                    in_=s_of[(b, ic, h)].rearrange("i (t p) -> i t p", t=PACK),
                     func=ACT.Exp,
                     bias=bias[:, x : x + 1],
                     scale=SCALE,

@@ -155,7 +155,10 @@ def tile_causalselfattention_t_kernel(tc, qkv, out):
 
         def copy_qk(b, h):
             qt = work.tile([P, 2 * NCH, P], BF16, tag="qkT%d" % h)
-            nc.vector.tensor_copy(out=qt[:], in_=tq_of[(b, h)][:])
+            if h == 0:
+                nc.vector.tensor_copy(out=qt[:], in_=tq_of[(b, h)][:])
+            else:
+                nc.scalar.copy(out=qt[:], in_=tq_of[(b, h)][:])
             qkT[(b, h)] = qt
 
         def one_score(b, h, ic, dst):

@@ -100,6 +100,7 @@ def tile_causalselfattention_t_kernel(tc, qkv, out):
         lq = {}
         stat = {}
         s_of = {}
+        tile_of = {}
         xt_of = {}
         g_of = {}
         ew_of = {}
@@ -161,43 +162,47 @@ def tile_causalselfattention_t_kernel(tc, qkv, out):
                 nc.scalar.copy(out=qt[:], in_=tq_of[(b, h)][:])
             qkT[(b, h)] = qt
 
+        def plain(dst, lhsT, rhs, first):
+            return lambda: nc.tensor.matmul(out=dst, lhsT=lhsT, rhs=rhs, start=first, stop=not first)
+
+        def transposition(dst, src):
+            return lambda: nc.tensor.transpose(out=dst, in_=src, identity=ident[:])
+
         def one_score(b, h, ic, dst):
             qt = qkT[(b, h)]
             live = QUAD * (ic + 1)
             dst3 = dst.rearrange("i (t p) -> i t p", t=PACK)
-            nc.tensor.matmul(
-                out=dst3,
-                lhsT=qt[:, ic, :],
-                rhs=qt[:, NCH : NCH + PACK, 0:live],
-                start=True,
-                stop=False,
-            )
-            nc.tensor.matmul(
-                out=dst3[:, :, live - QUAD : live], lhsT=ident[:], rhs=maskb[:], start=False, stop=True
-            )
+            return [
+                plain(dst3, qt[:, ic, :], qt[:, NCH : NCH + PACK, 0:live], True),
+                plain(dst3[:, :, live - QUAD : live], ident[:], maskb[:], False),
+            ]
 
-        def scores(n):
+        def score_matmuls(n):
             b, g = divmod(n, GROUPS)
             if g == 0:
                 nm = small.tile([P, NX], F32, tag="nm")
                 bias = small.tile([P, NX], F32, tag="bias")
                 rs = small.tile([P, NX], F32, tag="rs")
                 stat[b] = [nm, bias, rs]
-            nm, bias, rs = stat[b][0:3]
+            todo = []
             for k in range(2):
                 if g == 0:
-                    ic = k
-                    x0, x1 = ic * H, (ic + 1) * H
-                    s_ps = ps_s.tile([P, H, P * (ic + 1)], F32, tag="s")
+                    s_ps = ps_s.tile([P, H, P * (k + 1)], F32, tag="s")
                     for h in range(H):
-                        one_score(b, h, ic, s_ps[:, h, :])
-                        s_of[(b, ic, h)] = s_ps[:, h, :]
+                        todo.extend(one_score(b, h, k, s_ps[:, h, :]))
+                        s_of[(b, k, h)] = s_ps[:, h, :]
+                    tile_of[(n, k)] = (s_ps, k * H, (k + 1) * H)
                 else:
-                    ic = g + 1
-                    x0, x1 = ic * H + k, ic * H + k + 1
-                    s_ps = ps_s.tile([P, P * (ic + 1)], F32, tag="s")
-                    one_score(b, k, ic, s_ps[:])
-                    s_of[(b, ic, k)] = s_ps[:]
+                    s_ps = ps_s.tile([P, P * (g + 2)], F32, tag="s")
+                    todo.extend(one_score(b, k, g + 1, s_ps[:]))
+                    s_of[(b, g + 1, k)] = s_ps[:]
+                    tile_of[(n, k)] = (s_ps, (g + 1) * H + k, (g + 1) * H + k + 1)
+            return todo
+
+        def maxima(n):
+            nm, bias, rs = stat[n // GROUPS][0:3]
+            for k in range(2):
+                s_ps, x0, x1 = tile_of[(n, k)]
                 nc.vector.tensor_reduce(
                     out=nm[:, x0:x1], in_=s_ps[:], axis=AX.X, op=ALU.max, negate=True
                 )
@@ -209,6 +214,17 @@ def tile_causalselfattention_t_kernel(tc, qkv, out):
                     op0=ALU.mult,
                     op1=ALU.add,
                 )
+
+        def weave(mats, trs):
+            done = 0
+            for i in range(len(mats)):
+                mats[i]()
+                upto = (len(trs) * (i + 1)) // len(mats)
+                for tr in trs[done:upto]:
+                    tr()
+                done = upto
+            for tr in trs[done:]:
+                tr()
 
         def exps(n):
             b, g = divmod(n, GROUPS)
@@ -229,17 +245,15 @@ def tile_causalselfattention_t_kernel(tc, qkv, out):
                     accum_out=rs[:, x : x + 1],
                 )
 
-        def transpose_e(n):
+        def e_transposes(n):
             b, g = divmod(n, GROUPS)
             xt = ps_xt.tile([P, 2, PACK, P], BF16, tag="xt")
-            for k in range(2):
-                for t in range(PACK):
-                    nc.tensor.transpose(
-                        out=xt[:, k, t, :],
-                        in_=e_tiles[b % NSET][2 * g + k][:, t, :],
-                        identity=ident[:],
-                    )
             xt_of[n] = xt
+            return [
+                transposition(xt[:, k, t, :], e_tiles[b % NSET][2 * g + k][:, t, :])
+                for k in range(2)
+                for t in range(PACK)
+            ]
 
         def copy_out(n):
             grp = work.tile([P, 2, P, PACK], BF16, tag="grp", bufs=3, align_bytes=64)
@@ -326,12 +340,15 @@ def tile_causalselfattention_t_kernel(tc, qkv, out):
                 copy_qk(b0 + 2, 0)
             if r == 2 and batch_ok(b0 + 2):
                 copy_qk(b0 + 2, 1)
+            weave(
+                score_matmuls(n + 2) if 0 <= n + 2 < NG else [],
+                e_transposes(n) if 0 <= n < NG else [],
+            )
             if 0 <= n + 2 < NG:
-                scores(n + 2)
+                maxima(n + 2)
             if 0 <= n + 1 < NG:
                 exps(n + 1)
             if 0 <= n < NG:
-                transpose_e(n)
                 copy_out(n)
             if 0 <= n - 2 < NG:
                 passes(n - 2)

@@ -206,14 +206,13 @@ def tile_causalselfattention_t_kernel(tc, qkv, out):
                 nc.vector.tensor_reduce(
                     out=nm[:, x0:x1], in_=s_ps[:], axis=AX.X, op=ALU.max, negate=True
                 )
-                nc.gpsimd.tensor_scalar(
-                    out=bias[:, x0:x1],
-                    in0=nm[:, x0:x1],
-                    scalar1=SCALE,
-                    scalar2=0.0,
-                    op0=ALU.mult,
-                    op1=ALU.add,
-                )
+
+        def biases(n):
+            b, g = divmod(n, GROUPS)
+            nm, bias, rs = stat[b][0:3]
+            x0 = units(g)[0][0] * H
+            x1 = x0 + len(units(g))
+            nc.scalar.mul(out=bias[:, x0:x1], in_=nm[:, x0:x1], mul=SCALE)
 
         def weave(mats, trs):
             done = 0
@@ -348,6 +347,8 @@ def tile_causalselfattention_t_kernel(tc, qkv, out):
                 maxima(n + 2)
             if 0 <= n + 1 < NG:
                 exps(n + 1)
+            if 0 <= n + 2 < NG:
+                biases(n + 2)
             if 0 <= n < NG:
                 copy_out(n)
             if 0 <= n - 2 < NG:

@@ -90,13 +90,13 @@ def tile_causalselfattention_t_kernel(tc, qkv, out):
                     nc.vector.memset(e_t[:, :, 3 * QUAD : P], 0.0)
                 row.append(e_t)
             e_tiles.append(row)
-        vg = const.tile([P, H * D, PACK], BF16, name="vg", align_bytes=64)
         glo = const.tile([P, H, D, PACK], BF16, name="glo", align_bytes=64)
         nc.vector.memset(glo[:].rearrange("p x d t -> p (x d t)").bitcast(I32), 0)
 
         qkT = {}
         tq_of = {}
         vq = {}
+        vg_of = {}
         lq = {}
         stat = {}
         s_of = {}
@@ -118,29 +118,41 @@ def tile_causalselfattention_t_kernel(tc, qkv, out):
             )
 
         def regroup_full(b):
-            regroup(vg[:], kv_sb[b][:, :, H * D : 2 * H * D].rearrange("p t c -> p c t"))
-
-        def regroup_low(b):
-            regroup(
-                glo[0:HALF, 0, :, :], kv_sb[b][0:HALF, :, H * D : H * D + D].rearrange("p t d -> p d t")
+            vg = work.tile([P, H * D, PACK], BF16, tag="vg", align_bytes=64)
+            nc.vector.tensor_copy(
+                out=vg[:].rearrange("p (c i) t -> p c t i", i=PACK),
+                in_=kv_sb[b][:, :, H * D : 2 * H * D].rearrange("p t (c i) -> p c t i", i=PACK),
             )
-            regroup(glo[HALF:P, 1, :, :], vlo_sb[b][HALF:P, :, :].rearrange("p t d -> p d t"))
+            vg_of[b] = vg
+
+        def regroup_low(b, h):
+            if h == 0:
+                src = kv_sb[b][0:HALF, :, H * D : H * D + D]
+            else:
+                src = vlo_sb[b][HALF:P, :, :]
+            regroup(glo[h * HALF : (h + 1) * HALF, h, :, :], src.rearrange("p t d -> p d t"))
 
         def quantise_full(b):
             vw = work.tile([P, H * D], U32, tag="vw", bufs=3, align_bytes=64)
             vp = work.tile([P, H * D], U8, tag="vp", bufs=3, align_bytes=64)
             nc.vector.quantize_mx(
-                out=vw[:].bitcast(FP8X4), scales=vp[:], in_=vg[:].rearrange("p c t -> p (c t)")
+                out=vw[:].bitcast(FP8X4),
+                scales=vp[:],
+                in_=vg_of[b][:].rearrange("p c t -> p (c t)"),
             )
             vq[b] = [vw, vp]
 
-        def quantise_low(b):
-            lw = work.tile([P, H * D], U32, tag="lw", align_bytes=64)
-            lp = work.tile([P, H * D], U8, tag="lp", align_bytes=64)
+        def quantise_low(b, h):
+            if h == 0:
+                lw = work.tile([P, H * D], U32, tag="lw", align_bytes=64)
+                lp = work.tile([P, H * D], U8, tag="lp", align_bytes=64)
+                lq[b] = [lw, lp]
+            lw, lp = lq[b]
             nc.vector.quantize_mx(
-                out=lw[:].bitcast(FP8X4), scales=lp[:], in_=glo[:].rearrange("p x d t -> p (x d t)")
+                out=lw[:, h * D : (h + 1) * D].bitcast(FP8X4),
+                scales=lp[:, h * D : (h + 1) * D],
+                in_=glo[:, h, :, :].rearrange("p d t -> p (d t)"),
             )
-            lq[b] = [lw, lp]
 
         def transpose_qk(b, h):
             tq = ps_tq.tile([P, 2 * NCH, P], BF16, tag="tq")
@@ -319,22 +331,22 @@ def tile_causalselfattention_t_kernel(tc, qkv, out):
         def batch_ok(b):
             return 0 <= b < B
 
-        regroup_full(0)
-        regroup_low(0)
+        regroup_low(0, 0)
+        regroup_low(0, 1)
         for n in range(-6, NG + 3):
             b0, r = divmod(n, GROUPS)
             if 0 <= n - 3 < NG:
                 normalise(n - 3)
+            if r == 2 and batch_ok(b0 + 1):
+                quantise_full(b0 + 1)
+            if r > 0 and batch_ok(b0 + 1):
+                quantise_low(b0 + 1, r - 1)
+                if batch_ok(b0 + 2):
+                    regroup_low(b0 + 2, r - 1)
             if 0 <= n - 2 < NG:
                 quantise_e(n - 2)
-            if r == 1 and batch_ok(b0 + 1):
-                quantise_full(b0 + 1)
-                if batch_ok(b0 + 2):
-                    regroup_full(b0 + 2)
-            if r == 2 and batch_ok(b0 + 1):
-                quantise_low(b0 + 1)
-                if batch_ok(b0 + 2):
-                    regroup_low(b0 + 2)
+            if r == 0 and batch_ok(b0 + 1):
+                regroup_full(b0 + 1)
             if r == 1 and batch_ok(b0 + 2):
                 copy_qk(b0 + 2, 0)
             if r == 2 and batch_ok(b0 + 2):

@@ -90,13 +90,13 @@ def tile_causalselfattention_t_kernel(tc, qkv, out):
                     nc.vector.memset(e_t[:, :, 3 * QUAD : P], 0.0)
                 row.append(e_t)
             e_tiles.append(row)
+        vg = const.tile([P, H * D, PACK], BF16, name="vg", align_bytes=64)
         glo = const.tile([P, H, D, PACK], BF16, name="glo", align_bytes=64)
         nc.vector.memset(glo[:].rearrange("p x d t -> p (x d t)").bitcast(I32), 0)
 
         qkT = {}
         tq_of = {}
         vq = {}
-        vg_of = {}
         lq = {}
         stat = {}
         s_of = {}
@@ -118,12 +118,7 @@ def tile_causalselfattention_t_kernel(tc, qkv, out):
             )
 
         def regroup_full(b):
-            vg = work.tile([P, H * D, PACK], BF16, tag="vg", align_bytes=64)
-            nc.vector.tensor_copy(
-                out=vg[:].rearrange("p (c i) t -> p c t i", i=PACK),
-                in_=kv_sb[b][:, :, H * D : 2 * H * D].rearrange("p t (c i) -> p c t i", i=PACK),
-            )
-            vg_of[b] = vg
+            regroup(vg[:], kv_sb[b][:, :, H * D : 2 * H * D].rearrange("p t c -> p c t"))
 
         def regroup_low(b, h):
             if h == 0:
@@ -136,9 +131,7 @@ def tile_causalselfattention_t_kernel(tc, qkv, out):
             vw = work.tile([P, H * D], U32, tag="vw", bufs=3, align_bytes=64)
             vp = work.tile([P, H * D], U8, tag="vp", bufs=3, align_bytes=64)
             nc.vector.quantize_mx(
-                out=vw[:].bitcast(FP8X4),
-                scales=vp[:],
-                in_=vg_of[b][:].rearrange("p c t -> p (c t)"),
+                out=vw[:].bitcast(FP8X4), scales=vp[:], in_=vg[:].rearrange("p c t -> p (c t)")
             )
             vq[b] = [vw, vp]
 
@@ -225,17 +218,6 @@ def tile_causalselfattention_t_kernel(tc, qkv, out):
             x0 = units(g)[0][0] * H
             x1 = x0 + len(units(g))
             nc.scalar.mul(out=bias[:, x0:x1], in_=nm[:, x0:x1], mul=SCALE)
-
-        def weave(mats, trs):
-            done = 0
-            for i in range(len(mats)):
-                mats[i]()
-                upto = (len(trs) * (i + 1)) // len(mats)
-                for tr in trs[done:upto]:
-                    tr()
-                done = upto
-            for tr in trs[done:]:
-                tr()
 
         def exps(n):
             b, g = divmod(n, GROUPS)
@@ -331,32 +313,38 @@ def tile_causalselfattention_t_kernel(tc, qkv, out):
         def batch_ok(b):
             return 0 <= b < B
 
+        regroup_full(0)
         regroup_low(0, 0)
         regroup_low(0, 1)
         for n in range(-6, NG + 3):
             b0, r = divmod(n, GROUPS)
             if 0 <= n - 3 < NG:
                 normalise(n - 3)
-            if r == 2 and batch_ok(b0 + 1):
+            if r == 1 and batch_ok(b0 + 1):
                 quantise_full(b0 + 1)
-            if r > 0 and batch_ok(b0 + 1):
-                quantise_low(b0 + 1, r - 1)
                 if batch_ok(b0 + 2):
-                    regroup_low(b0 + 2, r - 1)
+                    regroup_full(b0 + 2)
+            if r == 2 and batch_ok(b0 + 1):
+                quantise_low(b0 + 1, 0)
+                if batch_ok(b0 + 2):
+                    regroup_low(b0 + 2, 0)
+            if r == 0 and batch_ok(b0):
+                quantise_low(b0, 1)
+                if batch_ok(b0 + 1):
+                    regroup_low(b0 + 1, 1)
             if 0 <= n - 2 < NG:
                 quantise_e(n - 2)
-            if r == 0 and batch_ok(b0 + 1):
-                regroup_full(b0 + 1)
             if r == 1 and batch_ok(b0 + 2):
                 copy_qk(b0 + 2, 0)
             if r == 2 and batch_ok(b0 + 2):
                 copy_qk(b0 + 2, 1)
-            weave(
-                score_matmuls(n + 2) if 0 <= n + 2 < NG else [],
-                e_transposes(n) if 0 <= n < NG else [],
-            )
             if 0 <= n + 2 < NG:
+                for matmul in score_matmuls(n + 2):
+                    matmul()
                 maxima(n + 2)
+            if 0 <= n < NG:
+                for transposition_of_e in e_transposes(n):
+                    transposition_of_e()
             if 0 <= n + 1 < NG:
                 exps(n + 1)
             if 0 <= n + 2 < NG:

@@ -64,6 +64,8 @@ def tile_causalselfattention_t_kernel(tc, qkv, out):
 
         ident = const.tile([P, P], BF16, name="ident")
         make_identity(nc, ident[:])
+        identf = const.tile([P, P], F32, name="identf")
+        make_identity(nc, identf[:])
         maskf = const.tile([P, P], F32, name="maskf")
         nc.gpsimd.memset(maskf[:], 0.0)
         nc.gpsimd.affine_select(
@@ -82,12 +84,12 @@ def tile_causalselfattention_t_kernel(tc, qkv, out):
         for s_i in range(NSET):
             row = []
             for k in range(2 * GROUPS):
-                e_t = const.tile([P, PACK, P], BF16, name="e_%d_%d" % (s_i, k))
+                e_t = const.tile([P, 2, P, 2], BF16, name="e_%d_%d" % (s_i, k))
                 if k == 0:
-                    nc.vector.memset(e_t[:, :, QUAD:HALF], 0.0)
-                    nc.vector.memset(e_t[:, :, HALF + QUAD : P], 0.0)
+                    nc.vector.memset(e_t[:, :, QUAD:HALF, :], 0.0)
+                    nc.vector.memset(e_t[:, :, HALF + QUAD : P, :], 0.0)
                 if k in (2, 3):
-                    nc.vector.memset(e_t[:, :, 3 * QUAD : P], 0.0)
+                    nc.vector.memset(e_t[:, :, 3 * QUAD : P, :], 0.0)
                 row.append(e_t)
             e_tiles.append(row)
         vg = const.tile([P, H * D, PACK], BF16, name="vg", align_bytes=64)
@@ -171,7 +173,7 @@ def tile_causalselfattention_t_kernel(tc, qkv, out):
             return lambda: nc.tensor.matmul(out=dst, lhsT=lhsT, rhs=rhs, start=first, stop=not first)
 
         def transposition(dst, src):
-            return lambda: nc.tensor.transpose(out=dst, in_=src, identity=ident[:])
+            return lambda: nc.tensor.transpose(out=dst, in_=src, identity=identf[:])
 
         def one_score(b, h, ic, dst):
             qt = qkT[(b, h)]
@@ -226,12 +228,12 @@ def tile_causalselfattention_t_kernel(tc, qkv, out):
                 x = ic * H + h
                 live = QUAD * (ic + 1)
                 if g == 0:
-                    dst = e_tiles[b % NSET][ic][:, :, h * HALF : h * HALF + live]
+                    dst = e_tiles[b % NSET][ic][:, :, h * HALF : h * HALF + live, :]
                 else:
-                    dst = e_tiles[b % NSET][2 * g + h][:, :, 0:live]
+                    dst = e_tiles[b % NSET][2 * g + h][:, :, 0:live, :]
                 nc.scalar.activation(
                     out=dst,
-                    in_=s_of[(b, ic, h)].rearrange("i (t p) -> i t p", t=PACK),
+                    in_=s_of[(b, ic, h)].rearrange("i (u w p) -> i u p w", u=2, w=2),
                     func=ACT.Exp,
                     bias=bias[:, x : x + 1],
                     scale=SCALE,
@@ -240,17 +242,20 @@ def tile_causalselfattention_t_kernel(tc, qkv, out):
 
         def e_transposes(n):
             b, g = divmod(n, GROUPS)
-            xt = ps_xt.tile([P, 2, PACK, P], BF16, tag="xt")
+            xt = ps_xt.tile([P, 2, 2, P], F32, tag="xt")
             xt_of[n] = xt
             return [
-                transposition(xt[:, k, t, :], e_tiles[b % NSET][2 * g + k][:, t, :])
+                transposition(
+                    xt[:, k, u, :],
+                    e_tiles[b % NSET][2 * g + k][:, u, :, :].rearrange("i p w -> i (p w)").bitcast(F32),
+                )
                 for k in range(2)
-                for t in range(PACK)
+                for u in range(2)
             ]
 
         def copy_out(n):
-            grp = work.tile([P, 2, P, PACK], BF16, tag="grp", bufs=3, align_bytes=64)
-            nc.scalar.copy(out=grp[:], in_=xt_of[n][:].rearrange("p x t i -> p x i t"))
+            grp = work.tile([P, 2, P, 2], F32, tag="grp", bufs=3, align_bytes=64)
+            nc.scalar.copy(out=grp[:], in_=xt_of[n][:].rearrange("p x u i -> p x i u"))
             g_of[n] = grp
 
         def quantise_e(n):
@@ -259,7 +264,7 @@ def tile_causalselfattention_t_kernel(tc, qkv, out):
             nc.vector.quantize_mx(
                 out=ew[:].bitcast(FP8X4),
                 scales=ep[:],
-                in_=g_of[n][:].rearrange("p x i t -> p (x i t)"),
+                in_=g_of[n][:].rearrange("p x i u -> p (x i u)").bitcast(BF16),
             )
             ew_of[n] = [ew, ep]
 

@@ -297,7 +297,7 @@ def tile_causalselfattention_t_kernel(tc, qkv, out):
                 rinv = small.tile([P, NX], F32, tag="rinv")
                 nc.vector.reciprocal(out=rinv[:], in_=stat[b][2][:])
                 stat[b].append(rinv)
-                o_sb = work.tile([P, NX, D], F32, tag="o_sb")
+                o_sb = work.tile([P, NX, D], F32, tag="o_sb", bufs=6)
                 osb_of[b] = o_sb
             rinv = stat[b][3]
             o_sb = osb_of[b]

@@ -163,7 +163,7 @@ def tile_causalselfattention_t_kernel(tc, qkv, out):
 
         def copy_qk(b, h):
             qt = work.tile([P, 2 * NCH, P], BF16, tag="qkT%d" % h)
-            if h == 0:
+            if h == 0 and b % 2 == 0:
                 nc.vector.tensor_copy(out=qt[:], in_=tq_of[(b, h)][:])
             else:
                 nc.scalar.copy(out=qt[:], in_=tq_of[(b, h)][:])
@@ -291,12 +291,14 @@ def tile_causalselfattention_t_kernel(tc, qkv, out):
                 )
             o_of[n] = o_ps
 
+        def reciprocals(b):
+            rinv = small.tile([P, NX], F32, tag="rinv")
+            nc.vector.reciprocal(out=rinv[:], in_=stat[b][2][:])
+            stat[b].append(rinv)
+
         def normalise(n):
             b, g = divmod(n, GROUPS)
             if g == 0:
-                rinv = small.tile([P, NX], F32, tag="rinv")
-                nc.vector.reciprocal(out=rinv[:], in_=stat[b][2][:])
-                stat[b].append(rinv)
                 o_sb = work.tile([P, NX, D], F32, tag="o_sb", bufs=6)
                 osb_of[b] = o_sb
             rinv = stat[b][3]
@@ -323,8 +325,10 @@ def tile_causalselfattention_t_kernel(tc, qkv, out):
         regroup_low(0, 1)
         for n in range(-6, NG + 3):
             b0, r = divmod(n, GROUPS)
-            if 0 <= n - 3 < NG:
-                normalise(n - 3)
+            if r == 0 and batch_ok(b0 - 1):
+                reciprocals(b0 - 1)
+            if 0 <= n - 2 < NG:
+                quantise_e(n - 2)
             if r == 1 and batch_ok(b0 + 1):
                 quantise_full(b0 + 1)
                 if batch_ok(b0 + 2):
@@ -337,12 +341,10 @@ def tile_causalselfattention_t_kernel(tc, qkv, out):
                 quantise_low(b0, 1)
                 if batch_ok(b0 + 1):
                     regroup_low(b0 + 1, 1)
-            if 0 <= n - 2 < NG:
-                quantise_e(n - 2)
+            if 0 <= n - 3 < NG:
+                normalise(n - 3)
             if r == 1 and batch_ok(b0 + 2):
                 copy_qk(b0 + 2, 0)
-            if r == 2 and batch_ok(b0 + 2):
-                copy_qk(b0 + 2, 1)
             if 0 <= n + 2 < NG:
                 for matmul in score_matmuls(n + 2):
                     matmul()
@@ -352,10 +354,12 @@ def tile_causalselfattention_t_kernel(tc, qkv, out):
                     transposition_of_e()
             if 0 <= n + 1 < NG:
                 exps(n + 1)
-            if 0 <= n + 2 < NG:
-                biases(n + 2)
             if 0 <= n < NG:
                 copy_out(n)
+            if r == 2 and batch_ok(b0 + 2):
+                copy_qk(b0 + 2, 1)
+            if 0 <= n + 2 < NG:
+                biases(n + 2)
             if 0 <= n - 2 < NG:
                 passes(n - 2)
             if r == 0 and batch_ok(b0 + 2):

@@ -25,6 +25,8 @@ NG = GROUPS * B
 SCALE = D ** -0.5
 NEG = -1.0e9
 NSET = 2
+NV = 3
+AHEAD = 3
 FLOPS = 4 * B * H * S * S * D
 
 
@@ -41,10 +43,10 @@ def tile_causalselfattention_t_kernel(tc, qkv, out):
         ps_xt = ctx.enter_context(tc.psum_pool(name="ps_xt", bufs=2))
         ps_o = ctx.enter_context(tc.psum_pool(name="ps_o", bufs=1))
 
-        q_sb = []
-        kv_sb = []
-        vlo_sb = []
-        for b in range(B):
+        q_sb = {}
+        kv_sb = {}
+
+        def load(b):
             q = inp.tile([P, NCH, H * D], BF16, tag="q")
             nc.sync.dma_start(
                 out=q[:], in_=qkv[b, :, 0, :, :].rearrange("(c p) h d -> p c (h d)", p=P)
@@ -53,14 +55,11 @@ def tile_causalselfattention_t_kernel(tc, qkv, out):
             nc.sync.dma_start(
                 out=kv[:], in_=qkv[b, :, 1:3, :, :].rearrange("(p t) w h d -> p t (w h d)", t=PACK)
             )
-            vlo = inp.tile([P, PACK, D], BF16, tag="vlo")
-            nc.sync.dma_start(
-                out=vlo[HALF:P, :, :],
-                in_=qkv[b, 0 : HALF * PACK, 2, 1, :].rearrange("(p t) d -> p t d", t=PACK),
-            )
-            q_sb.append(q)
-            kv_sb.append(kv)
-            vlo_sb.append(vlo)
+            q_sb[b] = q
+            kv_sb[b] = kv
+
+        for b in range(AHEAD):
+            load(b)
 
         ident = const.tile([P, P], BF16, name="ident")
         make_identity(nc, ident[:])
@@ -93,8 +92,19 @@ def tile_causalselfattention_t_kernel(tc, qkv, out):
                 row.append(e_t)
             e_tiles.append(row)
         vg = const.tile([P, H * D, PACK], BF16, name="vg", align_bytes=64)
-        glo = const.tile([P, H, D, PACK], BF16, name="glo", align_bytes=64)
-        nc.vector.memset(glo[:].rearrange("p x d t -> p (x d t)").bitcast(I32), 0)
+        v_tiles = []
+        for s_i in range(NV):
+            vw = const.tile([P, H * D], U32, name="vw_%d" % s_i, align_bytes=64)
+            vp = const.tile([P, H * D], U8, name="vp_%d" % s_i, align_bytes=64)
+            nc.vector.memset(vp[:].bitcast(I32), 0)
+            v_tiles.append([vw, vp])
+        low_tiles = []
+        for s_i in range(NSET):
+            lw = const.tile([P, H * D], U32, name="lw_%d" % s_i, align_bytes=64)
+            lp = const.tile([P, H * D], U8, name="lp_%d" % s_i, align_bytes=64)
+            nc.vector.memset(lw[:].bitcast(I32), 0)
+            nc.vector.memset(lp[:].bitcast(I32), 0)
+            low_tiles.append([lw, lp])
 
         qkT = {}
         tq_of = {}
@@ -122,32 +132,21 @@ def tile_causalselfattention_t_kernel(tc, qkv, out):
         def regroup_full(b):
             regroup(vg[:], kv_sb[b][:, :, H * D : 2 * H * D].rearrange("p t c -> p c t"))
 
-        def regroup_low(b, h):
-            if h == 0:
-                src = kv_sb[b][0:HALF, :, H * D : H * D + D]
-            else:
-                src = vlo_sb[b][HALF:P, :, :]
-            regroup(glo[h * HALF : (h + 1) * HALF, h, :, :], src.rearrange("p t d -> p d t"))
-
         def quantise_full(b):
-            vw = work.tile([P, H * D], U32, tag="vw", bufs=3, align_bytes=64)
-            vp = work.tile([P, H * D], U8, tag="vp", bufs=3, align_bytes=64)
+            vw, vp = v_tiles[b % NV]
             nc.vector.quantize_mx(
                 out=vw[:].bitcast(FP8X4), scales=vp[:], in_=vg[:].rearrange("p c t -> p (c t)")
             )
             vq[b] = [vw, vp]
 
-        def quantise_low(b, h):
-            if h == 0:
-                lw = work.tile([P, H * D], U32, tag="lw", align_bytes=64)
-                lp = work.tile([P, H * D], U8, tag="lp", align_bytes=64)
-                lq[b] = [lw, lp]
-            lw, lp = lq[b]
-            nc.vector.quantize_mx(
-                out=lw[:, h * D : (h + 1) * D].bitcast(FP8X4),
-                scales=lp[:, h * D : (h + 1) * D],
-                in_=glo[:, h, :, :].rearrange("p d t -> p (d t)"),
-            )
+        def copy_low(b):
+            for src, dst in zip(vq[b], low_tiles[b % NSET]):
+                for h in range(H):
+                    nc.sync.dma_start(
+                        out=dst[h * HALF : (h + 1) * HALF, h * D : (h + 1) * D].bitcast(I32),
+                        in_=src[0:HALF, h * D : (h + 1) * D].bitcast(I32),
+                    )
+            lq[b] = low_tiles[b % NSET]
 
         def transpose_qk(b, h):
             tq = ps_tq.tile([P, 2 * NCH, P], BF16, tag="tq")
@@ -321,26 +320,19 @@ def tile_causalselfattention_t_kernel(tc, qkv, out):
             return 0 <= b < B
 
         regroup_full(0)
-        regroup_low(0, 0)
-        regroup_low(0, 1)
         for n in range(-6, NG + 3):
             b0, r = divmod(n, GROUPS)
+            if r == 0 and batch_ok(b0 + 2 + AHEAD):
+                load(b0 + 2 + AHEAD)
             if r == 0 and batch_ok(b0 - 1):
                 reciprocals(b0 - 1)
             if 0 <= n - 2 < NG:
                 quantise_e(n - 2)
             if r == 1 and batch_ok(b0 + 1):
                 quantise_full(b0 + 1)
+                copy_low(b0 + 1)
                 if batch_ok(b0 + 2):
                     regroup_full(b0 + 2)
-            if r == 2 and batch_ok(b0 + 1):
-                quantise_low(b0 + 1, 0)
-                if batch_ok(b0 + 2):
-                    regroup_low(b0 + 2, 0)
-            if r == 0 and batch_ok(b0):
-                quantise_low(b0, 1)
-                if batch_ok(b0 + 1):
-                    regroup_low(b0 + 1, 1)
             if 0 <= n - 3 < NG:
                 normalise(n - 3)
             if r == 1 and batch_ok(b0 + 2):

@@ -337,6 +337,8 @@ def tile_causalselfattention_t_kernel(tc, qkv, out):
                 normalise(n - 3)
             if r == 1 and batch_ok(b0 + 2):
                 copy_qk(b0 + 2, 0)
+            if r == 2 and batch_ok(b0 + 2):
+                copy_qk(b0 + 2, 1)
             if 0 <= n + 2 < NG:
                 for matmul in score_matmuls(n + 2):
                     matmul()
@@ -346,12 +348,10 @@ def tile_causalselfattention_t_kernel(tc, qkv, out):
                     transposition_of_e()
             if 0 <= n + 1 < NG:
                 exps(n + 1)
-            if 0 <= n < NG:
-                copy_out(n)
-            if r == 2 and batch_ok(b0 + 2):
-                copy_qk(b0 + 2, 1)
             if 0 <= n + 2 < NG:
                 biases(n + 2)
+            if 0 <= n < NG:
+                copy_out(n)
             if 0 <= n - 2 < NG:
                 passes(n - 2)
             if r == 0 and batch_ok(b0 + 2):

@@ -48,13 +48,20 @@ def tile_causalselfattention_t_kernel(tc, qkv, out):
 
         def load(b):
             q = inp.tile([P, NCH, H * D], BF16, tag="q")
-            nc.sync.dma_start(
-                out=q[:], in_=qkv[b, :, 0, :, :].rearrange("(c p) h d -> p c (h d)", p=P)
-            )
             kv = inp.tile([P, PACK, 2 * H * D], BF16, tag="kv")
-            nc.sync.dma_start(
-                out=kv[:], in_=qkv[b, :, 1:3, :, :].rearrange("(p t) w h d -> p t (w h d)", t=PACK)
-            )
+            q_src = qkv[b, :, 0, :, :].rearrange("(c p) h d -> p c (h d)", p=P)
+            if b == 0:
+                nc.sync.dma_start(out=q[:], in_=q_src)
+                for w in range(2):
+                    nc.sync.dma_start(
+                        out=kv[:, :, w * H * D : (w + 1) * H * D],
+                        in_=qkv[b, :, 1 + w, :, :].rearrange("(p t) h d -> p t (h d)", t=PACK),
+                    )
+            else:
+                nc.sync.dma_start(out=q[:], in_=q_src)
+                nc.sync.dma_start(
+                    out=kv[:], in_=qkv[b, :, 1:3, :, :].rearrange("(p t) w h d -> p t (w h d)", t=PACK)
+                )
             q_sb[b] = q
             kv_sb[b] = kv
 
@@ -149,7 +156,10 @@ def tile_causalselfattention_t_kernel(tc, qkv, out):
             lq[b] = low_tiles[b % NSET]
 
         def transpose_qk(b, h):
-            tq = ps_tq.tile([P, 2 * NCH, P], BF16, tag="tq")
+            if (b, h) == (0, 1):
+                tq = ps_xt.tile([P, 2 * NCH, P], BF16, tag="xt")
+            else:
+                tq = ps_tq.tile([P, 2 * NCH, P], BF16, tag="tq")
             for c in range(NCH):
                 nc.tensor.transpose(
                     out=tq[:, c, :], in_=q_sb[b][:, c, h * D : (h + 1) * D], identity=ident[:]
@@ -218,7 +228,9 @@ def tile_causalselfattention_t_kernel(tc, qkv, out):
             nm, bias, rs = stat[b][0:3]
             x0 = units(g)[0][0] * H
             x1 = x0 + len(units(g))
-            nc.scalar.mul(out=bias[:, x0:x1], in_=nm[:, x0:x1], mul=SCALE)
+            nc.gpsimd.tensor_scalar(
+                out=bias[:, x0:x1], in0=nm[:, x0:x1], scalar1=SCALE, scalar2=0.0, op0=ALU.mult, op1=ALU.add
+            )
 
         def exps(n):
             b, g = divmod(n, GROUPS)
@@ -253,19 +265,29 @@ def tile_causalselfattention_t_kernel(tc, qkv, out):
             ]
 
         def copy_out(n):
-            grp = work.tile([P, 2, P, 2], F32, tag="grp", bufs=3, align_bytes=64)
-            nc.scalar.copy(out=grp[:], in_=xt_of[n][:].rearrange("p x u i -> p x i u"))
+            g = n % GROUPS
+            if g == 0:
+                grp = work.tile([P, 2, P, 2], F32, tag="grp0", align_bytes=64)
+            elif g == 1:
+                grp = work.tile([P, 4, P, 2], F32, tag="grp12", align_bytes=64)
+            else:
+                grp = g_of[n - 1]
+            x0 = 2 if g == 2 else 0
+            nc.scalar.copy(out=grp[:, x0 : x0 + 2, :, :], in_=xt_of[n][:].rearrange("p x u i -> p x i u"))
             g_of[n] = grp
 
         def quantise_e(n):
-            ew = work.tile([P, 2 * P], U32, tag="ew", align_bytes=64)
-            ep = work.tile([P, 2 * P], U8, tag="ep", align_bytes=64)
+            tiles = 2 if n % GROUPS == 0 else 4
+            ew = work.tile([P, tiles * P], U32, tag="ew%d" % tiles, align_bytes=64)
+            ep = work.tile([P, tiles * P], U8, tag="ep%d" % tiles, align_bytes=64)
             nc.vector.quantize_mx(
                 out=ew[:].bitcast(FP8X4),
                 scales=ep[:],
                 in_=g_of[n][:].rearrange("p x i u -> p (x i u)").bitcast(BF16),
             )
             ew_of[n] = [ew, ep]
+            if tiles == 4:
+                ew_of[n - 1] = [ew, ep]
 
         def passes(n):
             b, g = divmod(n, GROUPS)
@@ -273,16 +295,20 @@ def tile_causalselfattention_t_kernel(tc, qkv, out):
             vw, vp = vq[b]
             lw, lp = lq[b]
             width = H * D if g == 0 else D
-            o_ps = ps_o.tile([P, 2 * width], F32, tag="o")
+            if g == 2:
+                o_ps = o_of[n - 1]
+            else:
+                o_ps = ps_o.tile([P, 2 * H * D], F32, tag="o")
+            first = 2 if g == 2 else 0
             for k in range(2):
                 if g == 0:
                     rhs, rhs_scale = lw[:], lp[:]
                 else:
                     rhs, rhs_scale = vw[:, k * D : (k + 1) * D], vp[:, k * D : (k + 1) * D]
                 nc.tensor.matmul_mx(
-                    out=o_ps[:, k * width : (k + 1) * width],
-                    lhsT=ew[:, k * P : (k + 1) * P].bitcast(FP8X4),
-                    lhsT_scale=ep[:, k * P : (k + 1) * P],
+                    out=o_ps[:, (first + k) * width : (first + k + 1) * width],
+                    lhsT=ew[:, (first + k) * P : (first + k + 1) * P].bitcast(FP8X4),
+                    lhsT_scale=ep[:, (first + k) * P : (first + k + 1) * P],
                     rhs=rhs.bitcast(FP8X4),
                     rhs_scale=rhs_scale,
                     start=True,
@@ -302,19 +328,29 @@ def tile_causalselfattention_t_kernel(tc, qkv, out):
                 osb_of[b] = o_sb
             rinv = stat[b][3]
             o_sb = osb_of[b]
-            x0 = units(g)[0][0] * H
-            n_x = len(units(g))
+            x0 = 0 if g == 0 else NX // 2
+            n_x = NX // 2
             nc.vector.tensor_tensor(
                 out=o_sb[:, x0 : x0 + n_x, :],
                 in0=o_of[n][:].rearrange("p (x d) -> p x d", d=D),
                 in1=rinv[:, x0 : x0 + n_x].unsqueeze(2).to_broadcast([P, n_x, D]),
                 op=ALU.mult,
             )
-            if g == GROUPS - 1:
+            c1 = (x0 + n_x) // H
+            c0 = x0 // H if b == B - 1 else 0
+            if g == GROUPS - 1 or b == B - 1:
                 nc.sync.dma_start(
-                    out=out[b].rearrange("(c p) h d -> p c (h d)", p=P),
-                    in_=o_sb[:].rearrange("p (c h) d -> p c (h d)", h=H),
+                    out=out[b].rearrange("(c p) h d -> p c (h d)", p=P)[:, c0:c1, :],
+                    in_=o_sb[:].rearrange("p (c h) d -> p c (h d)", h=H)[:, c0:c1, :],
                 )
+
+        def qk_round(b, h):
+            return (GROUPS * (b - 2) if b != 1 else -2) + h
+
+        qk_at = {}
+        for b in range(B):
+            for h in range(H):
+                qk_at[qk_round(b, h)] = (b, h)
 
         def batch_ok(b):
             return 0 <= b < B
@@ -326,19 +362,17 @@ def tile_causalselfattention_t_kernel(tc, qkv, out):
                 load(b0 + 2 + AHEAD)
             if r == 0 and batch_ok(b0 - 1):
                 reciprocals(b0 - 1)
-            if 0 <= n - 2 < NG:
+            if 0 <= n - 2 < NG and r != 0:
                 quantise_e(n - 2)
-            if r == 1 and batch_ok(b0 + 1):
+            if r == 0 and batch_ok(b0 + 1):
                 quantise_full(b0 + 1)
                 copy_low(b0 + 1)
                 if batch_ok(b0 + 2):
                     regroup_full(b0 + 2)
-            if 0 <= n - 3 < NG:
+            if 0 <= n - 3 < NG and r != 1:
                 normalise(n - 3)
-            if r == 1 and batch_ok(b0 + 2):
-                copy_qk(b0 + 2, 0)
-            if r == 2 and batch_ok(b0 + 2):
-                copy_qk(b0 + 2, 1)
+            if n - 1 in qk_at:
+                copy_qk(qk_at[n - 1][0], qk_at[n - 1][1])
             if 0 <= n + 2 < NG:
                 for matmul in score_matmuls(n + 2):
                     matmul()
@@ -352,9 +386,9 @@ def tile_causalselfattention_t_kernel(tc, qkv, out):
                 biases(n + 2)
             if 0 <= n < NG:
                 copy_out(n)
-            if 0 <= n - 2 < NG:
+            if 0 <= n - 2 < NG and r == 1:
+                passes(n - 3)
+            if 0 <= n - 2 < NG and r != 0:
                 passes(n - 2)
-            if r == 0 and batch_ok(b0 + 2):
-                transpose_qk(b0 + 2, 0)
-            if r == 1 and batch_ok(b0 + 2):
-                transpose_qk(b0 + 2, 1)
+            if n in qk_at:
+                transpose_qk(qk_at[n][0], qk_at[n][1])

@@ -21,7 +21,6 @@ QUAD = P // PACK
 HALF = P // 2
 NX = NCH * H
 GROUPS = 3
-NG = GROUPS * B
 SCALE = D ** -0.5
 NEG = -1.0e9
 NSET = 2
@@ -113,6 +112,38 @@ def tile_causalselfattention_t_kernel(tc, qkv, out):
             nc.vector.memset(lp[:].bitcast(I32), 0)
             low_tiles.append([lw, lp])
 
+        low = [[(0, 0), (0, 1)], [(1, 0), (1, 1)]]
+        high = [[[(ic, 0)], [(ic, 1)]] for ic in (2, 3)]
+        groups = []
+        units = []
+        for b in range(B):
+            first = len(groups)
+            if b < B - 1:
+                groups.extend([(b, low), (b, high[0]), (b, high[1])])
+                units.extend([(b, first, first, 0, 2), (b, first + 1, first + 2, 2, 4)])
+            else:
+                groups.extend([(b, high[1]), (b, high[0]), (b, low[1:2]), (b, low[0:1])])
+                units.extend([(b, first, first + 1, 2, 4), (b, first + 2, first + 2, 1, 1), (b, first + 3, first + 3, 0, 1)])
+        NG = len(groups)
+        first_group = {}
+        for n in range(NG):
+            first_group.setdefault(groups[n][0], n)
+        unit_of = {}
+        ends_at = {}
+        for u in units:
+            for n in range(u[1], u[2] + 1):
+                unit_of[n] = u
+            if u[0] < B - 1:
+                ends_at[u[2]] = u
+
+        def e_index(tile):
+            ic, h = tile[0]
+            return ic if ic < 2 else 2 * (ic - 1) + h
+
+        def x_range(tiles):
+            xs = [ic * H + h for tile in tiles for ic, h in tile]
+            return min(xs), max(xs) + 1
+
         qkT = {}
         tq_of = {}
         vq = {}
@@ -125,11 +156,6 @@ def tile_causalselfattention_t_kernel(tc, qkv, out):
         ew_of = {}
         o_of = {}
         osb_of = {}
-
-        def units(g):
-            if g == 0:
-                return [(0, 0), (0, 1), (1, 0), (1, 1)]
-            return [(g + 1, 0), (g + 1, 1)]
 
         def regroup(dst, src):
             nc.gpsimd.tensor_scalar(
@@ -175,170 +201,147 @@ def tile_causalselfattention_t_kernel(tc, qkv, out):
             if h == 0 and b % 2 == 0:
                 nc.vector.tensor_copy(out=qt[:], in_=tq_of[(b, h)][:])
             else:
-                nc.scalar.copy(out=qt[:], in_=tq_of[(b, h)][:])
+                nc.scalar.copy(out=qt[:].bitcast(F32), in_=tq_of[(b, h)][:].bitcast(F32))
             qkT[(b, h)] = qt
-
-        def plain(dst, lhsT, rhs, first):
-            return lambda: nc.tensor.matmul(out=dst, lhsT=lhsT, rhs=rhs, start=first, stop=not first)
-
-        def transposition(dst, src):
-            return lambda: nc.tensor.transpose(out=dst, in_=src, identity=identf[:])
 
         def one_score(b, h, ic, dst):
             qt = qkT[(b, h)]
             live = QUAD * (ic + 1)
             dst3 = dst.rearrange("i (t p) -> i t p", t=PACK)
-            return [
-                plain(dst3, qt[:, ic, :], qt[:, NCH : NCH + PACK, 0:live], True),
-                plain(dst3[:, :, live - QUAD : live], ident[:], maskb[:], False),
-            ]
+            nc.tensor.matmul(out=dst3, lhsT=qt[:, ic, :], rhs=qt[:, NCH : NCH + PACK, 0:live], start=True, stop=False)
+            nc.tensor.matmul(out=dst3[:, :, live - QUAD : live], lhsT=ident[:], rhs=maskb[:], start=False, stop=True)
 
-        def score_matmuls(n):
-            b, g = divmod(n, GROUPS)
-            if g == 0:
+        def scores(n):
+            b, tiles = groups[n]
+            if n == first_group[b]:
                 nm = small.tile([P, NX], F32, tag="nm")
                 bias = small.tile([P, NX], F32, tag="bias")
                 rs = small.tile([P, NX], F32, tag="rs")
                 stat[b] = [nm, bias, rs]
-            todo = []
-            for k in range(2):
-                if g == 0:
-                    s_ps = ps_s.tile([P, H, P * (k + 1)], F32, tag="s")
-                    for h in range(H):
-                        todo.extend(one_score(b, h, k, s_ps[:, h, :]))
-                        s_of[(b, k, h)] = s_ps[:, h, :]
-                    tile_of[(n, k)] = (s_ps, k * H, (k + 1) * H)
-                else:
-                    s_ps = ps_s.tile([P, P * (g + 2)], F32, tag="s")
-                    todo.extend(one_score(b, k, g + 1, s_ps[:]))
-                    s_of[(b, g + 1, k)] = s_ps[:]
-                    tile_of[(n, k)] = (s_ps, (g + 1) * H + k, (g + 1) * H + k + 1)
-            return todo
+            for k, tile in enumerate(tiles):
+                cols = P * (tile[0][0] + 1)
+                s_ps = ps_s.tile([P, len(tile), cols], F32, tag="s")
+                for j, (ic, h) in enumerate(tile):
+                    one_score(b, h, ic, s_ps[:, j, :])
+                    s_of[(b, ic, h)] = s_ps[:, j, :]
+                tile_of[(n, k)] = s_ps
 
         def maxima(n):
-            nm, bias, rs = stat[n // GROUPS][0:3]
-            for k in range(2):
-                s_ps, x0, x1 = tile_of[(n, k)]
-                nc.vector.tensor_reduce(
-                    out=nm[:, x0:x1], in_=s_ps[:], axis=AX.X, op=ALU.max, negate=True
-                )
+            b, tiles = groups[n]
+            nm = stat[b][0]
+            for k, tile in enumerate(tiles):
+                x0, x1 = x_range([tile])
+                nc.vector.tensor_reduce(out=nm[:, x0:x1], in_=tile_of[(n, k)][:], axis=AX.X, op=ALU.max, negate=True)
 
         def biases(n):
-            b, g = divmod(n, GROUPS)
+            b, tiles = groups[n]
             nm, bias, rs = stat[b][0:3]
-            x0 = units(g)[0][0] * H
-            x1 = x0 + len(units(g))
+            x0, x1 = x_range(tiles)
             nc.gpsimd.tensor_scalar(
                 out=bias[:, x0:x1], in0=nm[:, x0:x1], scalar1=SCALE, scalar2=0.0, op0=ALU.mult, op1=ALU.add
             )
 
         def exps(n):
-            b, g = divmod(n, GROUPS)
+            b, tiles = groups[n]
             nm, bias, rs = stat[b][0:3]
-            for ic, h in units(g):
-                x = ic * H + h
-                live = QUAD * (ic + 1)
-                if g == 0:
-                    dst = e_tiles[b % NSET][ic][:, :, h * HALF : h * HALF + live, :]
-                else:
-                    dst = e_tiles[b % NSET][2 * g + h][:, :, 0:live, :]
-                nc.scalar.activation(
-                    out=dst,
-                    in_=s_of[(b, ic, h)].rearrange("i (u w p) -> i u p w", u=2, w=2),
-                    func=ACT.Exp,
-                    bias=bias[:, x : x + 1],
-                    scale=SCALE,
-                    accum_out=rs[:, x : x + 1],
-                )
+            for tile in tiles:
+                for ic, h in tile:
+                    x = ic * H + h
+                    live = QUAD * (ic + 1)
+                    p0 = h * HALF if ic < 2 else 0
+                    nc.scalar.activation(
+                        out=e_tiles[b % NSET][e_index(tile)][:, :, p0 : p0 + live, :],
+                        in_=s_of[(b, ic, h)].rearrange("i (u w p) -> i u p w", u=2, w=2),
+                        func=ACT.Exp,
+                        bias=bias[:, x : x + 1],
+                        scale=SCALE,
+                        accum_out=rs[:, x : x + 1],
+                    )
 
         def e_transposes(n):
-            b, g = divmod(n, GROUPS)
+            b, tiles = groups[n]
             xt = ps_xt.tile([P, 2, 2, P], F32, tag="xt")
             xt_of[n] = xt
-            return [
-                transposition(
-                    xt[:, k, u, :],
-                    e_tiles[b % NSET][2 * g + k][:, u, :, :].rearrange("i p w -> i (p w)").bitcast(F32),
-                )
-                for k in range(2)
-                for u in range(2)
-            ]
+            for k, tile in enumerate(tiles):
+                for u in range(2):
+                    nc.tensor.transpose(
+                        out=xt[:, k, u, :],
+                        in_=e_tiles[b % NSET][e_index(tile)][:, u, :, :].rearrange("i p w -> i (p w)").bitcast(F32),
+                        identity=identf[:],
+                    )
 
         def copy_out(n):
-            g = n % GROUPS
-            if g == 0:
-                grp = work.tile([P, 2, P, 2], F32, tag="grp0", align_bytes=64)
-            elif g == 1:
-                grp = work.tile([P, 4, P, 2], F32, tag="grp12", align_bytes=64)
-            else:
-                grp = g_of[n - 1]
-            x0 = 2 if g == 2 else 0
-            nc.scalar.copy(out=grp[:, x0 : x0 + 2, :, :], in_=xt_of[n][:].rearrange("p x u i -> p x i u"))
-            g_of[n] = grp
+            b, tiles = groups[n]
+            u = unit_of[n]
+            if u not in g_of:
+                grp = work.tile([P, u[4], P, 2], F32, tag="grp%d" % u[4], align_bytes=64)
+                g_of[u] = grp
+            x0 = e_index(tiles[0]) - u[3]
+            nc.scalar.copy(
+                out=g_of[u][:, x0 : x0 + len(tiles), :, :],
+                in_=xt_of[n][:, 0 : len(tiles), :, :].rearrange("p x u i -> p x i u"),
+            )
 
-        def quantise_e(n):
-            tiles = 2 if n % GROUPS == 0 else 4
-            ew = work.tile([P, tiles * P], U32, tag="ew%d" % tiles, align_bytes=64)
-            ep = work.tile([P, tiles * P], U8, tag="ep%d" % tiles, align_bytes=64)
+        def quantise_e(u):
+            ew = work.tile([P, u[4] * P], U32, tag="ew%d" % u[4], align_bytes=64)
+            ep = work.tile([P, u[4] * P], U8, tag="ep%d" % u[4], align_bytes=64)
             nc.vector.quantize_mx(
                 out=ew[:].bitcast(FP8X4),
                 scales=ep[:],
-                in_=g_of[n][:].rearrange("p x i u -> p (x i u)").bitcast(BF16),
+                in_=g_of[u][:].rearrange("p x i u -> p (x i u)").bitcast(BF16),
             )
-            ew_of[n] = [ew, ep]
-            if tiles == 4:
-                ew_of[n - 1] = [ew, ep]
+            ew_of[u] = [ew, ep]
 
-        def passes(n):
-            b, g = divmod(n, GROUPS)
-            ew, ep = ew_of[n]
+        def passes(u):
+            b = u[0]
+            ew, ep = ew_of[u]
             vw, vp = vq[b]
             lw, lp = lq[b]
-            width = H * D if g == 0 else D
-            if g == 2:
-                o_ps = o_of[n - 1]
+            if u[4] == 1:
+                o_ps = ps_s.tile([P, 2 * H * D], F32, tag="s")
             else:
                 o_ps = ps_o.tile([P, 2 * H * D], F32, tag="o")
-            first = 2 if g == 2 else 0
-            for k in range(2):
-                if g == 0:
+            width = H * D if u[3] < 2 else D
+            for k in range(u[4]):
+                if u[3] < 2:
                     rhs, rhs_scale = lw[:], lp[:]
                 else:
-                    rhs, rhs_scale = vw[:, k * D : (k + 1) * D], vp[:, k * D : (k + 1) * D]
+                    h = (u[3] + k) % H
+                    rhs, rhs_scale = vw[:, h * D : (h + 1) * D], vp[:, h * D : (h + 1) * D]
                 nc.tensor.matmul_mx(
-                    out=o_ps[:, (first + k) * width : (first + k + 1) * width],
-                    lhsT=ew[:, (first + k) * P : (first + k + 1) * P].bitcast(FP8X4),
-                    lhsT_scale=ep[:, (first + k) * P : (first + k + 1) * P],
+                    out=o_ps[:, k * width : (k + 1) * width],
+                    lhsT=ew[:, k * P : (k + 1) * P].bitcast(FP8X4),
+                    lhsT_scale=ep[:, k * P : (k + 1) * P],
                     rhs=rhs.bitcast(FP8X4),
                     rhs_scale=rhs_scale,
                     start=True,
                     stop=True,
                 )
-            o_of[n] = o_ps
+            o_of[u] = o_ps
 
         def reciprocals(b):
             rinv = small.tile([P, NX], F32, tag="rinv")
             nc.vector.reciprocal(out=rinv[:], in_=stat[b][2][:])
             stat[b].append(rinv)
 
-        def normalise(n):
-            b, g = divmod(n, GROUPS)
-            if g == 0:
+        def normalise(u):
+            b = u[0]
+            if b not in osb_of:
                 o_sb = work.tile([P, NX, D], F32, tag="o_sb", bufs=6)
                 osb_of[b] = o_sb
             rinv = stat[b][3]
             o_sb = osb_of[b]
-            x0 = 0 if g == 0 else NX // 2
-            n_x = NX // 2
+            x0, x1 = x_range([tile for n in range(u[1], u[2] + 1) for tile in groups[n][1]])
+            n_x = x1 - x0
             nc.vector.tensor_tensor(
-                out=o_sb[:, x0 : x0 + n_x, :],
-                in0=o_of[n][:].rearrange("p (x d) -> p x d", d=D),
-                in1=rinv[:, x0 : x0 + n_x].unsqueeze(2).to_broadcast([P, n_x, D]),
+                out=o_sb[:, x0:x1, :],
+                in0=o_of[u][:, 0 : n_x * D].rearrange("p (x d) -> p x d", d=D),
+                in1=rinv[:, x0:x1].unsqueeze(2).to_broadcast([P, n_x, D]),
                 op=ALU.mult,
             )
-            c1 = (x0 + n_x) // H
+            c1 = x1 // H
             c0 = x0 // H if b == B - 1 else 0
-            if g == GROUPS - 1 or b == B - 1:
+            if x1 == NX or b == B - 1:
                 nc.sync.dma_start(
                     out=out[b].rearrange("(c p) h d -> p c (h d)", p=P)[:, c0:c1, :],
                     in_=o_sb[:].rearrange("p (c h) d -> p c (h d)", h=H)[:, c0:c1, :],
@@ -356,39 +359,43 @@ def tile_causalselfattention_t_kernel(tc, qkv, out):
             return 0 <= b < B
 
         regroup_full(0)
-        for n in range(-6, NG + 3):
+        for n in range(-6, NG):
             b0, r = divmod(n, GROUPS)
             if r == 0 and batch_ok(b0 + 2 + AHEAD):
                 load(b0 + 2 + AHEAD)
-            if r == 0 and batch_ok(b0 - 1):
+            if r == 0 and 0 <= b0 - 1 < B - 1:
                 reciprocals(b0 - 1)
-            if 0 <= n - 2 < NG and r != 0:
-                quantise_e(n - 2)
+            if n - 2 in ends_at:
+                quantise_e(ends_at[n - 2])
             if r == 0 and batch_ok(b0 + 1):
                 quantise_full(b0 + 1)
                 copy_low(b0 + 1)
                 if batch_ok(b0 + 2):
                     regroup_full(b0 + 2)
-            if 0 <= n - 3 < NG and r != 1:
-                normalise(n - 3)
+            if n - 3 in ends_at:
+                normalise(ends_at[n - 3])
             if n - 1 in qk_at:
                 copy_qk(qk_at[n - 1][0], qk_at[n - 1][1])
             if 0 <= n + 2 < NG:
-                for matmul in score_matmuls(n + 2):
-                    matmul()
+                scores(n + 2)
                 maxima(n + 2)
             if 0 <= n < NG:
-                for transposition_of_e in e_transposes(n):
-                    transposition_of_e()
+                e_transposes(n)
             if 0 <= n + 1 < NG:
                 exps(n + 1)
             if 0 <= n + 2 < NG:
                 biases(n + 2)
             if 0 <= n < NG:
                 copy_out(n)
-            if 0 <= n - 2 < NG and r == 1:
-                passes(n - 3)
-            if 0 <= n - 2 < NG and r != 0:
-                passes(n - 2)
+            if n - 2 in ends_at:
+                passes(ends_at[n - 2])
             if n in qk_at:
                 transpose_qk(qk_at[n][0], qk_at[n][1])
+        last = [u for u in units if u[0] == B - 1]
+        for u in last:
+            quantise_e(u)
+        for u in last:
+            passes(u)
+        reciprocals(B - 1)
+        for u in last:
+            normalise(u)

@@ -37,10 +37,8 @@ def tile_causalselfattention_t_kernel(tc, qkv, out):
         inp = ctx.enter_context(tc.tile_pool(name="inp", bufs=B))
         work = ctx.enter_context(tc.tile_pool(name="work", bufs=2))
         small = ctx.enter_context(tc.tile_pool(name="small", bufs=3))
-        ps_tq = ctx.enter_context(tc.psum_pool(name="ps_tq", bufs=1))
-        ps_s = ctx.enter_context(tc.psum_pool(name="ps_s", bufs=4))
-        ps_xt = ctx.enter_context(tc.psum_pool(name="ps_xt", bufs=2))
-        ps_o = ctx.enter_context(tc.psum_pool(name="ps_o", bufs=1))
+        ps_s = ctx.enter_context(tc.psum_pool(name="ps_s", bufs=5))
+        ps_xt = ctx.enter_context(tc.psum_pool(name="ps_xt", bufs=3))
 
         q_sb = {}
         kv_sb = {}
@@ -185,7 +183,7 @@ def tile_causalselfattention_t_kernel(tc, qkv, out):
             if (b, h) == (0, 1):
                 tq = ps_xt.tile([P, 2 * NCH, P], BF16, tag="xt")
             else:
-                tq = ps_tq.tile([P, 2 * NCH, P], BF16, tag="tq")
+                tq = ps_xt.tile([P, 2 * NCH, P], BF16, tag="xt")
             for c in range(NCH):
                 nc.tensor.transpose(
                     out=tq[:, c, :], in_=q_sb[b][:, c, h * D : (h + 1) * D], identity=ident[:]
@@ -300,7 +298,7 @@ def tile_causalselfattention_t_kernel(tc, qkv, out):
             if u[4] == 1:
                 o_ps = ps_s.tile([P, 2 * H * D], F32, tag="s")
             else:
-                o_ps = ps_o.tile([P, 2 * H * D], F32, tag="o")
+                o_ps = ps_xt.tile([P, 2 * H * D], F32, tag="xt")
             width = H * D if u[3] < 2 else D
             for k in range(u[4]):
                 if u[3] < 2:

@@ -160,8 +160,14 @@ def tile_causalselfattention_t_kernel(tc, qkv, out):
                 out=dst, in0=src, scalar1=1.0, scalar2=0.0, op0=ALU.mult, op1=ALU.add
             )
 
+        def regroup_head(b, h):
+            regroup(
+                vg[:, h * D : (h + 1) * D, :], kv_sb[b][:, :, (H + h) * D : (H + h + 1) * D].rearrange("p t c -> p c t")
+            )
+
         def regroup_full(b):
-            regroup(vg[:], kv_sb[b][:, :, H * D : 2 * H * D].rearrange("p t c -> p c t"))
+            for h in range(H):
+                regroup_head(b, h)
 
         def quantise_full(b):
             vw, vp = v_tiles[b % NV]
@@ -361,6 +367,8 @@ def tile_causalselfattention_t_kernel(tc, qkv, out):
             b0, r = divmod(n, GROUPS)
             if r == 0 and batch_ok(b0 + 2 + AHEAD):
                 load(b0 + 2 + AHEAD)
+            if r == 2 and n >= -GROUPS and batch_ok(b0 + 2):
+                regroup_head(b0 + 2, 1)
             if r == 0 and 0 <= b0 - 1 < B - 1:
                 reciprocals(b0 - 1)
             if n - 2 in ends_at:
@@ -369,7 +377,7 @@ def tile_causalselfattention_t_kernel(tc, qkv, out):
                 quantise_full(b0 + 1)
                 copy_low(b0 + 1)
                 if batch_ok(b0 + 2):
-                    regroup_full(b0 + 2)
+                    regroup_head(b0 + 2, 0)
             if n - 3 in ends_at:
                 normalise(ends_at[n - 3])
             if n - 1 in qk_at:

@@ -215,14 +215,16 @@ def tile_causalselfattention_t_kernel(tc, qkv, out):
             nc.tensor.matmul(out=dst3, lhsT=qt[:, ic, :], rhs=qt[:, NCH : NCH + PACK, 0:live], start=True, stop=False)
             nc.tensor.matmul(out=dst3[:, :, live - QUAD : live], lhsT=ident[:], rhs=maskb[:], start=False, stop=True)
 
-        def scores(n):
+        def scores(n, places):
             b, tiles = groups[n]
-            if n == first_group[b]:
+            if n == first_group[b] and 0 in places:
                 nm = small.tile([P, NX], F32, tag="nm")
                 bias = small.tile([P, NX], F32, tag="bias")
                 rs = small.tile([P, NX], F32, tag="rs")
                 stat[b] = [nm, bias, rs]
             for k, tile in enumerate(tiles):
+                if k not in places:
+                    continue
                 cols = P * (tile[0][0] + 1)
                 s_ps = ps_s.tile([P, len(tile), cols], F32, tag="s")
                 for j, (ic, h) in enumerate(tile):
@@ -362,6 +364,7 @@ def tile_causalselfattention_t_kernel(tc, qkv, out):
         def batch_ok(b):
             return 0 <= b < B
 
+        early = set()
         regroup_full(0)
         for n in range(-6, NG):
             b0, r = divmod(n, GROUPS)
@@ -383,7 +386,7 @@ def tile_causalselfattention_t_kernel(tc, qkv, out):
             if n - 1 in qk_at:
                 copy_qk(qk_at[n - 1][0], qk_at[n - 1][1])
             if 0 <= n + 2 < NG:
-                scores(n + 2)
+                scores(n + 2, [1] if n + 2 in early else [0, 1])
                 maxima(n + 2)
             if 0 <= n < NG:
                 e_transposes(n)
@@ -395,6 +398,9 @@ def tile_causalselfattention_t_kernel(tc, qkv, out):
                 copy_out(n)
             if n - 2 in ends_at:
                 passes(ends_at[n - 2])
+            if n - 2 in ends_at and n in qk_at and n + 3 < NG:
+                scores(n + 3, [0])
+                early.add(n + 3)
             if n in qk_at:
                 transpose_qk(qk_at[n][0], qk_at[n][1])
         last = [u for u in units if u[0] == B - 1]

@@ -121,7 +121,7 @@ def tile_causalselfattention_t_kernel(tc, qkv, out):
                 units.extend([(b, first, first, 0, 2), (b, first + 1, first + 2, 2, 4)])
             else:
                 groups.extend([(b, high[1]), (b, high[0]), (b, low[1:2]), (b, low[0:1])])
-                units.extend([(b, first, first + 1, 2, 4), (b, first + 2, first + 2, 1, 1), (b, first + 3, first + 3, 0, 1)])
+                units.extend([(b, first + j, first + j, e0, count) for j, (e0, count) in enumerate([(4, 2), (2, 2), (1, 1), (0, 1)])])
         NG = len(groups)
         first_group = {}
         for n in range(NG):
@@ -131,7 +131,7 @@ def tile_causalselfattention_t_kernel(tc, qkv, out):
         for u in units:
             for n in range(u[1], u[2] + 1):
                 unit_of[n] = u
-            if u[0] < B - 1:
+            if u[0] < B - 1 or u[3] == 4:
                 ends_at[u[2]] = u
 
         def e_index(tile):
@@ -325,10 +325,11 @@ def tile_causalselfattention_t_kernel(tc, qkv, out):
                 )
             o_of[u] = o_ps
 
-        def reciprocals(b):
-            rinv = small.tile([P, NX], F32, tag="rinv")
-            nc.vector.reciprocal(out=rinv[:], in_=stat[b][2][:])
-            stat[b].append(rinv)
+        def reciprocals(b, x0, x1):
+            if len(stat[b]) == 3:
+                rinv = small.tile([P, NX], F32, tag="rinv")
+                stat[b].append(rinv)
+            nc.vector.reciprocal(out=stat[b][3][:, x0:x1], in_=stat[b][2][:, x0:x1])
 
         def normalise(u):
             b = u[0]
@@ -373,7 +374,9 @@ def tile_causalselfattention_t_kernel(tc, qkv, out):
             if r == 2 and n >= -GROUPS and batch_ok(b0 + 2):
                 regroup_head(b0 + 2, 1)
             if r == 0 and 0 <= b0 - 1 < B - 1:
-                reciprocals(b0 - 1)
+                reciprocals(b0 - 1, 0, NX)
+            if n == NG - 1:
+                reciprocals(B - 1, NX - H, NX)
             if n - 2 in ends_at:
                 quantise_e(ends_at[n - 2])
             if r == 0 and batch_ok(b0 + 1):
@@ -403,11 +406,11 @@ def tile_causalselfattention_t_kernel(tc, qkv, out):
                 early.add(n + 3)
             if n in qk_at:
                 transpose_qk(qk_at[n][0], qk_at[n][1])
-        last = [u for u in units if u[0] == B - 1]
+        last = [u for u in units if u[0] == B - 1 and u[2] not in ends_at]
         for u in last:
             quantise_e(u)
         for u in last:
             passes(u)
-        reciprocals(B - 1)
+        reciprocals(B - 1, 0, NX - H)
         for u in last:
             normalise(u)

from contextlib import ExitStack

import concourse.mybir as mybir
from concourse.masks import make_identity

BF16 = mybir.dt.bfloat16
F32 = mybir.dt.float32
I32 = mybir.dt.int32
U32 = mybir.dt.uint32
U8 = mybir.dt.uint8
FP8X4 = mybir.dt.float8_e4m3fn_x4
ACT = mybir.ActivationFunctionType
ALU = mybir.AluOpType
AX = mybir.AxisListType

B, S, H, D = 16, 512, 2, 128
P = 128
NCH = S // P
PACK = 4
QUAD = P // PACK
HALF = P // 2
NX = NCH * H
GROUPS = 3
SCALE = D ** -0.5
NEG = -1.0e9
NSET = 2
NV = 3
AHEAD = 3
FLOPS = 4 * B * H * S * S * D


def tile_causalselfattention_t_kernel(tc, qkv, out):
    nc = tc.nc
    with ExitStack() as ctx:
        ctx.enter_context(tc.manual_schedule())
        const = ctx.enter_context(tc.tile_pool(name="const", bufs=1))
        inp = ctx.enter_context(tc.tile_pool(name="inp", bufs=B))
        work = ctx.enter_context(tc.tile_pool(name="work", bufs=2))
        small = ctx.enter_context(tc.tile_pool(name="small", bufs=3))
        ps_s = ctx.enter_context(tc.psum_pool(name="ps_s", bufs=5))
        ps_xt = ctx.enter_context(tc.psum_pool(name="ps_xt", bufs=3))

        q_sb = {}
        kv_sb = {}

        def load(b):
            q = inp.tile([P, NCH, H * D], BF16, tag="q")
            kv = inp.tile([P, PACK, 2 * H * D], BF16, tag="kv")
            q_src = qkv[b, :, 0, :, :].rearrange("(c p) h d -> p c (h d)", p=P)
            if b == 0:
                nc.sync.dma_start(out=q[:], in_=q_src)
                for w in range(2):
                    nc.sync.dma_start(
                        out=kv[:, :, w * H * D : (w + 1) * H * D],
                        in_=qkv[b, :, 1 + w, :, :].rearrange("(p t) h d -> p t (h d)", t=PACK),
                    )
            else:
                nc.sync.dma_start(out=q[:], in_=q_src)
                nc.sync.dma_start(
                    out=kv[:], in_=qkv[b, :, 1:3, :, :].rearrange("(p t) w h d -> p t (w h d)", t=PACK)
                )
            q_sb[b] = q
            kv_sb[b] = kv

        for b in range(AHEAD):
            load(b)

        ident = const.tile([P, P], BF16, name="ident")
        make_identity(nc, ident[:])
        identf = const.tile([P, P], F32, name="identf")
        make_identity(nc, identf[:])
        maskf = const.tile([P, P], F32, name="maskf")
        nc.gpsimd.memset(maskf[:], 0.0)
        nc.gpsimd.affine_select(
            out=maskf[:],
            in_=maskf[:],
            pattern=[[-1, P]],
            compare_op=ALU.is_ge,
            fill=NEG,
            base=0,
            channel_multiplier=1,
        )
        maskb = const.tile([P, PACK, QUAD], BF16, name="maskb")
        nc.vector.tensor_copy(out=maskb[:], in_=maskf[:].rearrange("i (p t) -> i t p", t=PACK))

        e_tiles = []
        for s_i in range(NSET):
            row = []
            for k in range(2 * GROUPS):
                e_t = const.tile([P, 2, P, 2], BF16, name="e_%d_%d" % (s_i, k))
                if k == 0:
                    nc.vector.memset(e_t[:, :, QUAD:HALF, :], 0.0)
                    nc.vector.memset(e_t[:, :, HALF + QUAD : P, :], 0.0)
                if k in (2, 3):
                    nc.vector.memset(e_t[:, :, 3 * QUAD : P, :], 0.0)
                row.append(e_t)
            e_tiles.append(row)
        vg = const.tile([P, H * D, PACK], BF16, name="vg", align_bytes=64)
        v_tiles = []
        for s_i in range(NV):
            vw = const.tile([P, H * D], U32, name="vw_%d" % s_i, align_bytes=64)
            vp = const.tile([P, H * D], U8, name="vp_%d" % s_i, align_bytes=64)
            nc.vector.memset(vp[:].bitcast(I32), 0)
            v_tiles.append([vw, vp])
        low_tiles = []
        for s_i in range(NSET):
            lw = const.tile([P, H * D], U32, name="lw_%d" % s_i, align_bytes=64)
            lp = const.tile([P, H * D], U8, name="lp_%d" % s_i, align_bytes=64)
            nc.vector.memset(lw[:].bitcast(I32), 0)
            nc.vector.memset(lp[:].bitcast(I32), 0)
            low_tiles.append([lw, lp])

        low = [[(0, 0), (0, 1)], [(1, 0), (1, 1)]]
        high = [[[(ic, 0)], [(ic, 1)]] for ic in (2, 3)]
        groups = []
        units = []
        for b in range(B):
            first = len(groups)
            if b < B - 1:
                groups.extend([(b, low), (b, high[0]), (b, high[1])])
                units.extend([(b, first, first, 0, 2), (b, first + 1, first + 2, 2, 4)])
            else:
                groups.extend([(b, high[1]), (b, high[0]), (b, low[1:2]), (b, low[0:1])])
                units.extend([(b, first + j, first + j, e0, count) for j, (e0, count) in enumerate([(4, 2), (2, 2), (1, 1), (0, 1)])])
        NG = len(groups)
        first_group = {}
        for n in range(NG):
            first_group.setdefault(groups[n][0], n)
        unit_of = {}
        ends_at = {}
        for u in units:
            for n in range(u[1], u[2] + 1):
                unit_of[n] = u
            if u[0] < B - 1 or u[3] == 4:
                ends_at[u[2]] = u

        def e_index(tile):
            ic, h = tile[0]
            return ic if ic < 2 else 2 * (ic - 1) + h

        def x_range(tiles):
            xs = [ic * H + h for tile in tiles for ic, h in tile]
            return min(xs), max(xs) + 1

        qkT = {}
        tq_of = {}
        vq = {}
        lq = {}
        stat = {}
        s_of = {}
        tile_of = {}
        xt_of = {}
        g_of = {}
        ew_of = {}
        o_of = {}
        osb_of = {}

        def regroup(dst, src):
            nc.gpsimd.tensor_scalar(
                out=dst, in0=src, scalar1=1.0, scalar2=0.0, op0=ALU.mult, op1=ALU.add
            )

        def regroup_head(b, h):
            regroup(
                vg[:, h * D : (h + 1) * D, :], kv_sb[b][:, :, (H + h) * D : (H + h + 1) * D].rearrange("p t c -> p c t")
            )

        def regroup_full(b):
            for h in range(H):
                regroup_head(b, h)

        def quantise_full(b):
            vw, vp = v_tiles[b % NV]
            nc.vector.quantize_mx(
                out=vw[:].bitcast(FP8X4), scales=vp[:], in_=vg[:].rearrange("p c t -> p (c t)")
            )
            vq[b] = [vw, vp]

        def copy_low(b):
            for src, dst in zip(vq[b], low_tiles[b % NSET]):
                for h in range(H):
                    nc.sync.dma_start(
                        out=dst[h * HALF : (h + 1) * HALF, h * D : (h + 1) * D].bitcast(I32),
                        in_=src[0:HALF, h * D : (h + 1) * D].bitcast(I32),
                    )
            lq[b] = low_tiles[b % NSET]

        def transpose_qk(b, h):
            if (b, h) == (0, 1):
                tq = ps_xt.tile([P, 2 * NCH, P], BF16, tag="xt")
            else:
                tq = ps_xt.tile([P, 2 * NCH, P], BF16, tag="xt")
            for c in range(NCH):
                nc.tensor.transpose(
                    out=tq[:, c, :], in_=q_sb[b][:, c, h * D : (h + 1) * D], identity=ident[:]
                )
            for t in range(PACK):
                nc.tensor.transpose(
                    out=tq[:, NCH + t, :], in_=kv_sb[b][:, t, h * D : (h + 1) * D], identity=ident[:]
                )
            tq_of[(b, h)] = tq

        def copy_qk(b, h):
            qt = work.tile([P, 2 * NCH, P], BF16, tag="qkT%d" % h)
            if h == 0 and b % 2 == 0:
                nc.vector.tensor_copy(out=qt[:], in_=tq_of[(b, h)][:])
            else:
                nc.scalar.copy(out=qt[:].bitcast(F32), in_=tq_of[(b, h)][:].bitcast(F32))
            qkT[(b, h)] = qt

        def one_score(b, h, ic, dst):
            qt = qkT[(b, h)]
            live = QUAD * (ic + 1)
            dst3 = dst.rearrange("i (t p) -> i t p", t=PACK)
            nc.tensor.matmul(out=dst3, lhsT=qt[:, ic, :], rhs=qt[:, NCH : NCH + PACK, 0:live], start=True, stop=False)
            nc.tensor.matmul(out=dst3[:, :, live - QUAD : live], lhsT=ident[:], rhs=maskb[:], start=False, stop=True)

        def scores(n, places):
            b, tiles = groups[n]
            if n == first_group[b] and 0 in places:
                nm = small.tile([P, NX], F32, tag="nm")
                bias = small.tile([P, NX], F32, tag="bias")
                rs = small.tile([P, NX], F32, tag="rs")
                stat[b] = [nm, bias, rs]
            for k, tile in enumerate(tiles):
                if k not in places:
                    continue
                cols = P * (tile[0][0] + 1)
                s_ps = ps_s.tile([P, len(tile), cols], F32, tag="s")
                for j, (ic, h) in enumerate(tile):
                    one_score(b, h, ic, s_ps[:, j, :])
                    s_of[(b, ic, h)] = s_ps[:, j, :]
                tile_of[(n, k)] = s_ps

        def maxima(n):
            b, tiles = groups[n]
            nm = stat[b][0]
            for k, tile in enumerate(tiles):
                x0, x1 = x_range([tile])
                nc.vector.tensor_reduce(out=nm[:, x0:x1], in_=tile_of[(n, k)][:], axis=AX.X, op=ALU.max, negate=True)

        def biases(n):
            b, tiles = groups[n]
            nm, bias, rs = stat[b][0:3]
            x0, x1 = x_range(tiles)
            nc.gpsimd.tensor_scalar(
                out=bias[:, x0:x1], in0=nm[:, x0:x1], scalar1=SCALE, scalar2=0.0, op0=ALU.mult, op1=ALU.add
            )

        def exps(n):
            b, tiles = groups[n]
            nm, bias, rs = stat[b][0:3]
            for tile in tiles:
                for ic, h in tile:
                    x = ic * H + h
                    live = QUAD * (ic + 1)
                    p0 = h * HALF if ic < 2 else 0
                    nc.scalar.activation(
                        out=e_tiles[b % NSET][e_index(tile)][:, :, p0 : p0 + live, :],
                        in_=s_of[(b, ic, h)].rearrange("i (u w p) -> i u p w", u=2, w=2),
                        func=ACT.Exp,
                        bias=bias[:, x : x + 1],
                        scale=SCALE,
                        accum_out=rs[:, x : x + 1],
                    )

        def e_transposes(n):
            b, tiles = groups[n]
            xt = ps_xt.tile([P, 2, 2, P], F32, tag="xt")
            xt_of[n] = xt
            for k, tile in enumerate(tiles):
                for u in range(2):
                    nc.tensor.transpose(
                        out=xt[:, k, u, :],
                        in_=e_tiles[b % NSET][e_index(tile)][:, u, :, :].rearrange("i p w -> i (p w)").bitcast(F32),
                        identity=identf[:],
                    )

        def copy_out(n):
            b, tiles = groups[n]
            u = unit_of[n]
            if u not in g_of:
                grp = work.tile([P, u[4], P, 2], F32, tag="grp%d" % u[4], align_bytes=64)
                g_of[u] = grp
            x0 = e_index(tiles[0]) - u[3]
            nc.scalar.copy(
                out=g_of[u][:, x0 : x0 + len(tiles), :, :],
                in_=xt_of[n][:, 0 : len(tiles), :, :].rearrange("p x u i -> p x i u"),
            )

        def quantise_e(u):
            ew = work.tile([P, u[4] * P], U32, tag="ew%d" % u[4], align_bytes=64)
            ep = work.tile([P, u[4] * P], U8, tag="ep%d" % u[4], align_bytes=64)
            nc.vector.quantize_mx(
                out=ew[:].bitcast(FP8X4),
                scales=ep[:],
                in_=g_of[u][:].rearrange("p x i u -> p (x i u)").bitcast(BF16),
            )
            ew_of[u] = [ew, ep]

        def passes(u):
            b = u[0]
            ew, ep = ew_of[u]
            vw, vp = vq[b]
            lw, lp = lq[b]
            if u[4] == 1:
                o_ps = ps_s.tile([P, 2 * H * D], F32, tag="s")
            else:
                o_ps = ps_xt.tile([P, 2 * H * D], F32, tag="xt")
            width = H * D if u[3] < 2 else D
            for k in range(u[4]):
                if u[3] < 2:
                    rhs, rhs_scale = lw[:], lp[:]
                else:
                    h = (u[3] + k) % H
                    rhs, rhs_scale = vw[:, h * D : (h + 1) * D], vp[:, h * D : (h + 1) * D]
                nc.tensor.matmul_mx(
                    out=o_ps[:, k * width : (k + 1) * width],
                    lhsT=ew[:, k * P : (k + 1) * P].bitcast(FP8X4),
                    lhsT_scale=ep[:, k * P : (k + 1) * P],
                    rhs=rhs.bitcast(FP8X4),
                    rhs_scale=rhs_scale,
                    start=True,
                    stop=True,
                )
            o_of[u] = o_ps

        def reciprocals(b, x0, x1):
            if len(stat[b]) == 3:
                rinv = small.tile([P, NX], F32, tag="rinv")
                stat[b].append(rinv)
            nc.vector.reciprocal(out=stat[b][3][:, x0:x1], in_=stat[b][2][:, x0:x1])

        def normalise(u):
            b = u[0]
            if b not in osb_of:
                o_sb = work.tile([P, NX, D], F32, tag="o_sb", bufs=6)
                osb_of[b] = o_sb
            rinv = stat[b][3]
            o_sb = osb_of[b]
            x0, x1 = x_range([tile for n in range(u[1], u[2] + 1) for tile in groups[n][1]])
            n_x = x1 - x0
            nc.vector.tensor_tensor(
                out=o_sb[:, x0:x1, :],
                in0=o_of[u][:, 0 : n_x * D].rearrange("p (x d) -> p x d", d=D),
                in1=rinv[:, x0:x1].unsqueeze(2).to_broadcast([P, n_x, D]),
                op=ALU.mult,
            )
            c1 = x1 // H
            c0 = x0 // H if b == B - 1 else 0
            if x1 == NX or b == B - 1:
                nc.sync.dma_start(
                    out=out[b].rearrange("(c p) h d -> p c (h d)", p=P)[:, c0:c1, :],
                    in_=o_sb[:].rearrange("p (c h) d -> p c (h d)", h=H)[:, c0:c1, :],
                )

        def qk_round(b, h):
            return (GROUPS * (b - 2) if b != 1 else -2) + h

        qk_at = {}
        for b in range(B):
            for h in range(H):
                qk_at[qk_round(b, h)] = (b, h)

        def batch_ok(b):
            return 0 <= b < B

        early = set()
        regroup_full(0)
        for n in range(-6, NG):
            b0, r = divmod(n, GROUPS)
            if r == 0 and batch_ok(b0 + 2 + AHEAD):
                load(b0 + 2 + AHEAD)
            if r == 2 and n >= -GROUPS and batch_ok(b0 + 2):
                regroup_head(b0 + 2, 1)
            if r == 0 and 0 <= b0 - 1 < B - 1:
                reciprocals(b0 - 1, 0, NX)
            if n == NG - 1:
                reciprocals(B - 1, NX - H, NX)
            if n - 2 in ends_at:
                quantise_e(ends_at[n - 2])
            if r == 0 and batch_ok(b0 + 1):
                quantise_full(b0 + 1)
                copy_low(b0 + 1)
                if batch_ok(b0 + 2):
                    regroup_head(b0 + 2, 0)
            if n - 3 in ends_at:
                normalise(ends_at[n - 3])
            if n - 1 in qk_at:
                copy_qk(qk_at[n - 1][0], qk_at[n - 1][1])
            if 0 <= n + 2 < NG:
                scores(n + 2, [1] if n + 2 in early else [0, 1])
                maxima(n + 2)
            if 0 <= n < NG:
                e_transposes(n)
            if 0 <= n + 1 < NG:
                exps(n + 1)
            if 0 <= n + 2 < NG:
                biases(n + 2)
            if 0 <= n < NG:
                copy_out(n)
            if n - 2 in ends_at:
                passes(ends_at[n - 2])
            if n - 2 in ends_at and n in qk_at and n + 3 < NG:
                scores(n + 3, [0])
                early.add(n + 3)
            if n in qk_at:
                transpose_qk(qk_at[n][0], qk_at[n][1])
        last = [u for u in units if u[0] == B - 1 and u[2] not in ends_at]
        for u in last:
            quantise_e(u)
        for u in last:
            passes(u)
        reciprocals(B - 1, 0, NX - H)
        for u in last:
            normalise(u)
